import numpy as np
import ml_dtypes


def mxq(x, axis, fmt="e4m3"):
    dtype, down = {"e4m3": (ml_dtypes.float8_e4m3fn, 7), "e5m2": (ml_dtypes.float8_e5m2, 14)}[fmt]
    v = np.moveaxis(np.asarray(x, np.float32).astype(ml_dtypes.bfloat16).astype(np.float64), axis, -1)
    blocks = v.reshape(v.shape[:-1] + (-1, 32))
    amax = np.abs(blocks).max(-1, keepdims=True)
    byte = np.maximum(np.where(amax > 0, np.frexp(amax)[1] - 1 + 127, 0) - down, 1)
    scale = np.exp2(byte - 127.0)
    codes = (blocks / scale).astype(np.float32).astype(dtype).astype(np.float64)
    return np.moveaxis((codes * scale).reshape(v.shape), -1, axis)


WIDE = False


def mx_kscale(k):
    if not WIDE:
        return np.ones(k)
    levels = np.array([10, -10, 5, -5, 0])
    a = np.random.permutation(np.resize(levels, k // 512 * 4)).reshape(k // 512, 4)
    idx = np.arange(k)
    return np.exp2(a[idx // 512, idx % 128 // 32])


BF16 = ml_dtypes.bfloat16


def bf(x):
    return np.asarray(x, np.float32).astype(BF16)


def f64(x):
    return np.asarray(x).astype(np.float64)


B, I, H, AH, AI, G = 512, 1024, 1024, 128, 128, 4
EPS = 1e-5


def sigmoid(v):
    return 1.0 / (1.0 + np.exp(-v))


def ln(v, w, b):
    mu = v.mean(-1, keepdims=True)
    var = ((v - mu) ** 2).mean(-1, keepdims=True)
    return (v - mu) / np.sqrt(var + EPS) * w + b


def setup_inputs():
    n = np.random.standard_normal
    s, t = mx_kscale(I), mx_kscale(H)
    return {
        "x": bf(n((B, I)) * s),
        "hx": bf(n((B, H)) * t),
        "cx": bf(n((B, H))),
        "zw": bf(1.0 + 0.5 * n((B, 2 * G, AI))),
        "zb": bf(0.7 * n((B, 2 * G, AI))),
        "w_ih": bf(n((G * H, I)) / np.sqrt(I) / s),
        "w_hh": bf(n((G * H, H)) / np.sqrt(H) / t),
        "b_ih": bf(0.2 * n(G * H)),
        "b_hh": bf(0.2 * n(G * H)),
        "norm_alpha_w": bf(n((2 * G, H, AI)) / np.sqrt(AI)),
        "bias_beta_w": bf(0.7 * n((2 * G, H, AI)) / np.sqrt(AI)),
        "ln_i_w": bf(1.0 + 0.1 * n(G * H)),
        "ln_i_b": bf(0.2 * n(G * H)),
        "ln_h_w": bf(1.0 + 0.1 * n(G * H)),
        "ln_h_b": bf(0.2 * n(G * H)),
        "ln_c_w": bf(1.0 + 0.1 * n(H)),
        "ln_c_b": bf(0.2 * n(H)),
    }


def reference(x, hx, cx, zw, zb, w_ih, w_hh, b_ih, b_hh, norm_alpha_w, bias_beta_w, ln_i_w, ln_i_b, ln_h_w, ln_h_b, ln_c_w, ln_c_b):
    alpha = (f64(zw).transpose(1, 0, 2) @ f64(norm_alpha_w).transpose(0, 2, 1)).transpose(1, 0, 2)
    beta = (f64(zb).transpose(1, 0, 2) @ f64(bias_beta_w).transpose(0, 2, 1)).transpose(1, 0, 2)
    xh = (mxq(f64(x), 1, "e4m3") @ mxq(f64(w_ih), 1, "e4m3").T).reshape(-1, G, H)
    hh = (mxq(f64(hx), 1, "e4m3") @ mxq(f64(w_hh), 1, "e4m3").T).reshape(-1, G, H)
    in_g = (xh * alpha[:, :G] + f64(b_ih).reshape(G, H) + beta[:, :G]).reshape(-1, G * H)
    hid_g = (hh * alpha[:, G:] + f64(b_hh).reshape(G, H) + beta[:, G:]).reshape(-1, G * H)
    gates = ln(in_g, f64(ln_i_w), f64(ln_i_b)) + ln(hid_g, f64(ln_h_w), f64(ln_h_b))
    i, j, f, o = np.split(gates, G, axis=1)
    cy = ln(sigmoid(f) * f64(cx) + sigmoid(i) * np.tanh(j), f64(ln_c_w), f64(ln_c_b))
    hy = sigmoid(o) * np.tanh(cy)
    return hy, cy

@@ -1,0 +1,435 @@
+from contextlib import ExitStack
+
+import concourse.mybir as mybir
+from concourse.masks import make_identity
+
+F32 = mybir.dt.float32
+BF16 = mybir.dt.bfloat16
+U32 = mybir.dt.uint32
+U8 = mybir.dt.uint8
+FP8X4 = mybir.dt.float8_e4m3fn_x4
+ALU = mybir.AluOpType
+ACT = mybir.ActivationFunctionType
+AX = mybir.AxisListType
+
+P = 128
+B = 512
+K = 1024
+H = 1024
+NB = B // P
+NCOL = 4 * H
+CH = 512
+NCH = NCOL // CH
+EPS = 1e-5
+LAG = 2
+PIN = False
+
+FLOPS = 2 * 2 * B * NCOL * K + 16 * 2 * B * H * 128
+
+
+def tile_adaptivelstmcell_pb_kernel(
+    tc, x, hx, cx, zw, zb, w_ih, w_hh, b_ih, b_hh, norm_alpha_w, bias_beta_w,
+    ln_i_w, ln_i_b, ln_h_w, ln_h_b, ln_c_w, ln_c_b, out_0, out_1,
+):
+    nc = tc.nc
+    with ExitStack() as ctx:
+        if PIN:
+            ctx.enter_context(tc.manual_schedule())
+        keep = ctx.enter_context(tc.tile_pool(name="keep", bufs=1))
+        cst = ctx.enter_context(tc.tile_pool(name="cst", bufs=2))
+        ps_tp = ctx.enter_context(tc.psum_pool(name="ps_tp", bufs=2))
+        ps_xh = ctx.enter_context(tc.psum_pool(name="ps_xh", bufs=2))
+        ps_al = ctx.enter_context(tc.psum_pool(name="ps_al", bufs=2))
+        ps_be = ctx.enter_context(tc.psum_pool(name="ps_be", bufs=2))
+
+        Ut = keep.tile([P, NB * NCOL], F32, name="Ut")
+        Vt = keep.tile([P, NB * NCOL], F32, name="Vt")
+        ident_f = keep.tile([P, P], F32, name="ident_f")
+        ident_b = keep.tile([P, P], BF16, name="ident_b")
+        xc = [keep.tile([P, 2, B], U32, name="xc%d" % h, align_bytes=64) for h in range(2)]
+        xs = [keep.tile([P, 2, B], U8, name="xs%d" % h, align_bytes=64) for h in range(2)]
+        zwT = keep.tile([P, 8, B], BF16, name="zwT")
+        zbT = keep.tile([P, 8, B], BF16, name="zbT")
+        Bz = keep.tile([P, CH], BF16, name="Bz")
+        Rw = keep.tile([P, 2, P], BF16, name="Rw")
+        cT = keep.tile([P, 2 * P], BF16, name="cT")
+        bsumT = keep.tile([P, 32], F32, name="bsumT")
+        neghalf = keep.tile([P, NB], F32, name="neghalf")
+        dmy = keep.tile([P, 1], F32, name="dmy")
+        sumU = keep.tile([P, 2, NB, NCH], F32, name="sumU")
+        sqU = keep.tile([P, 2, NB, NCH], F32, name="sqU")
+        bsm = keep.tile([P, NCH], F32, name="bsm")
+        btot = keep.tile([P, 1], F32, name="btot")
+        sumC = keep.tile([P, NB], F32, name="sumC")
+        sqC = keep.tile([P, NB], F32, name="sqC")
+        junk = keep.tile([P, H], BF16, name="junk")
+
+        def copy_on(eng, out, in_):
+            if eng == "s":
+                nc.scalar.copy(out=out, in_=in_)
+            else:
+                nc.vector.tensor_copy(out=out, in_=in_)
+
+        def stage_f(i):
+            return Vt[:, i * 2048:(i + 1) * 2048]
+
+        def stage_b(i):
+            return stage_f(i).bitcast(BF16).rearrange("p (r k) -> p r k", r=4)
+
+        def rows4(ap2d):
+            return ap2d.rearrange("(r p) k -> p r k", p=P)
+
+        nc.vector.memset(neghalf[:], -0.5)
+        nc.scalar.activation(out=dmy[:], in_=neghalf[:, 0:1], func=ACT.Sigmoid)
+        nc.vector.memset(Rw[:], 0.0)
+        nc.vector.memset(Bz[:], 0.0)
+        make_identity(nc, ident_f[:])
+        make_identity(nc, ident_b[:])
+
+        with ExitStack() as sctx:
+            rawp = sctx.enter_context(tc.tile_pool(name="rawp", bufs=2))
+            abp = sctx.enter_context(tc.tile_pool(name="abp", bufs=2))
+            grpp = sctx.enter_context(tc.tile_pool(name="grpp", bufs=3))
+            wqp = sctx.enter_context(tc.tile_pool(name="wqp", bufs=2))
+            wabp = sctx.enter_context(tc.tile_pool(name="wabp", bufs=2))
+            alp = sctx.enter_context(tc.tile_pool(name="alp", bufs=3))
+
+            def load_w(k):
+                w = w_ih if k < NCH else w_hh
+                c = k % NCH
+                raw = rawp.tile([P, 2048], F32, name="raww")
+                nc.sync.dma_start(
+                    out=raw[:].bitcast(BF16).rearrange("p (r k) -> p r k", r=4),
+                    in_=rows4(w[c * CH:(c + 1) * CH, :]),
+                )
+                return raw
+
+            def load_ab(s):
+                ra = abp.tile([P, 8, P], BF16, name="rawa")
+                rb = abp.tile([P, 8, P], BF16, name="rawb")
+                nc.sync.dma_start(out=ra[:], in_=norm_alpha_w[s, :, :].rearrange("(r p) a -> p r a", p=P))
+                nc.sync.dma_start(out=rb[:], in_=bias_beta_w[s, :, :].rearrange("(r p) a -> p r a", p=P))
+                return (ra, rb)
+
+            def mx_half(src, g, engs):
+                grp = grpp.tile([P, 2048], BF16, name="grp", align_bytes=64)
+                gview = grp[:].bitcast(F32).rearrange("p (n u) -> p n u", u=2)
+                for rp in range(2):
+                    bank = ps_tp.tile([P, 2, 2, P], F32, name="tpw", tag="tp")
+                    for u in range(2):
+                        for r2 in range(2):
+                            col = (2 * rp + r2) * 512 + 256 * g + 128 * u
+                            nc.tensor.transpose(bank[:, u, r2, :], src[:, col:col + P], ident_f[:])
+                    copy_on(engs[rp], gview[:, 256 * rp:256 * rp + 256, :],
+                            bank[:].rearrange("p u r c -> p (r c) u"))
+                return grp
+
+            def quant(grp, codes, scales, g):
+                nc.vector.quantize_mx(out=codes[:, g, :].bitcast(FP8X4), scales=scales[:, g, :], in_=grp[:])
+
+            def prep_z(i, dstT, s0, bp, eng):
+                srcb = stage_b(i)
+                bank = ps_tp.tile([P, 4, 2, P], BF16, name="tpz", tag="tp")
+                for s in range(4):
+                    for bl in range(2):
+                        nc.tensor.transpose(bank[:, s, bl, :],
+                                            srcb[:, 2 * bp + bl, (s0 + s) * P:(s0 + s + 1) * P], ident_b[:])
+                copy_on(eng, dstT[:, s0:s0 + 4, 256 * bp:256 * bp + 256],
+                        bank[:].rearrange("p s l b -> p s (l b)"))
+
+            def prep_wab(k, ab):
+                hh = k % 2
+                bank = ps_tp.tile([P, 2, 4, P], BF16, name="tpab", tag="tp")
+                for j in range(2):
+                    for r in range(4):
+                        nc.tensor.transpose(bank[:, j, r, :], ab[j][:, hh * 4 + r, :], ident_b[:])
+                wab = wabp.tile([P, 2, CH], BF16, name="wab")
+                nc.scalar.copy(out=wab[:], in_=bank[:].rearrange("p j r c -> p j (r c)"))
+                return wab
+
+            def bc_bf(col0, n):
+                bank = ps_tp.tile([P, n, P], BF16, name="tpc", tag="tp")
+                for j in range(n):
+                    nc.tensor.transpose(bank[:, j, :], cT[:, col0 + j:col0 + j + 1].to_broadcast([P, P]),
+                                        ident_b[:])
+                return bank
+
+            def prep_bias(c):
+                bank = bc_bf(4 * c, 4)
+                t = cst.tile([P, CH], BF16, name="biasbc")
+                nc.scalar.activation(out=t[:], in_=bank[:].rearrange("p j c -> p (j c)"), func=ACT.Copy,
+                                     accum_out=bsm[:, c:c + 1])
+                return t
+
+            def prep_w(col0, c):
+                bank = bc_bf(col0 + 4 * c, 4)
+                t = cst.tile([P, CH], BF16, name="wbc")
+                nc.scalar.copy(out=t[:], in_=bank[:].rearrange("p j c -> p (j c)"))
+                return t
+
+            def prep_bsum(c):
+                bank = ps_tp.tile([P, 4, P], F32, name="tpf", tag="tp")
+                for j in range(4):
+                    nc.tensor.transpose(bank[:, j, :],
+                                        bsumT[:, 4 * c + j:4 * c + j + 1].to_broadcast([P, P]), ident_f[:])
+                t = cst.tile([P, CH], F32, name="bsb")
+                nc.scalar.copy(out=t[:], in_=bank[:].rearrange("p j c -> p (j c)"))
+                return t
+
+            def finish_stats(nm, s1, s2, inv_n, shift):
+                mean = keep.tile([P, NB], F32, name="mean_" + nm)
+                msq = keep.tile([P, NB], F32, name="msq_" + nm)
+                var = keep.tile([P, NB], F32, name="var_" + nm)
+                rstd = keep.tile([P, NB], F32, name="rstd_" + nm)
+                if shift is None:
+                    nc.vector.tensor_scalar(out=mean[:], in0=s1, scalar1=inv_n, scalar2=None, op0=ALU.mult)
+                else:
+                    nc.vector.tensor_scalar(out=mean[:], in0=s1, scalar1=shift, scalar2=inv_n,
+                                            op0=ALU.add, op1=ALU.mult)
+                nc.vector.tensor_tensor(out=msq[:], in0=mean[:], in1=mean[:], op=ALU.mult)
+                nc.vector.scalar_tensor_tensor(out=var[:], in0=s2, scalar=inv_n, in1=msq[:],
+                                               op0=ALU.mult, op1=ALU.subtract)
+                nc.vector.tensor_scalar(out=var[:], in0=var[:], scalar1=0.0, scalar2=EPS,
+                                        op0=ALU.max, op1=ALU.add)
+                nc.gpsimd.tensor_tensor(out=rstd[:], in0=var[:], in1=neghalf[:], op=ALU.pow)
+                return (mean, rstd)
+
+            def half_stats(nm, half, shift):
+                s1 = keep.tile([P, NB], F32, name="s1_" + nm)
+                s2 = keep.tile([P, NB], F32, name="s2_" + nm)
+                nc.vector.tensor_reduce(out=s1[:], in_=sumU[:, half, :, :], axis=AX.X, op=ALU.add)
+                nc.vector.tensor_reduce(out=s2[:], in_=sqU[:, half, :, :], axis=AX.X, op=ALU.add)
+                return finish_stats(nm, s1[:], s2[:], 1.0 / NCOL, shift)
+
+            def seg_of(T, bt, c):
+                return T[:, bt * NCOL + c * CH:bt * NCOL + (c + 1) * CH]
+
+            zw2 = rows4(zw.rearrange("b s a -> b (s a)"))
+            zb2 = rows4(zb.rearrange("b s a -> b (s a)"))
+            raws = {}
+            abs_ = {}
+            nc.sync.dma_start(out=stage_b(0), in_=rows4(x))
+            raws[0] = load_w(0)
+            nc.sync.dma_start(out=stage_b(2)[:, :, 0:512], in_=zw2[:, :, 0:512])
+            nc.sync.dma_start(out=stage_b(3)[:, :, 0:512], in_=zb2[:, :, 0:512])
+            abs_[0] = load_ab(0)
+            for (gi, r0, vec) in ((0, 0, b_ih), (0, 32, ln_i_w), (0, 64, ln_h_w), (0, 96, ln_c_w),
+                                  (0, 104, ln_c_b), (1, 0, ln_i_b), (1, 32, ln_h_b)):
+                m = vec.shape[0] // P
+                nc.sync.dma_start(out=Rw[r0:r0 + m, gi, :], in_=vec.rearrange("(m p) -> m p", p=P))
+            nc.sync.dma_start(out=Bz[0:NCH, :], in_=b_hh.rearrange("(c n) -> c n", c=NCH))
+            raws[1] = load_w(1)
+            abs_[1] = load_ab(1)
+            nc.sync.dma_start(out=stage_b(1), in_=rows4(hx))
+            nc.sync.dma_start(out=stage_b(2)[:, :, 512:1024], in_=zw2[:, :, 512:1024])
+            nc.sync.dma_start(out=stage_b(3)[:, :, 512:1024], in_=zb2[:, :, 512:1024])
+
+            wcs = {}
+            wss = {}
+            wabs = {}
+            biases = {}
+            ficst = {}
+
+            def new_wq(k):
+                wcs[k] = wqp.tile([P, 2, CH], U32, name="wc", align_bytes=64)
+                wss[k] = wqp.tile([P, 2, CH], U8, name="ws", align_bytes=64)
+
+            g0 = mx_half(stage_f(0), 0, ("s", "v"))
+            g1 = mx_half(stage_f(0), 1, ("s", "v"))
+            quant(g0, xc[0], xs[0], 0)
+            new_wq(0)
+            g2 = mx_half(raws[0][:], 0, ("s", "v"))
+            quant(g1, xc[0], xs[0], 1)
+            g3 = mx_half(raws[0][:], 1, ("s", "v"))
+            quant(g2, wcs[0], wss[0], 0)
+            raws[2] = load_w(2)
+            prep_z(2, zwT, 0, 0, "s")
+            prep_z(2, zwT, 0, 1, "v")
+            quant(g3, wcs[0], wss[0], 1)
+            prep_z(3, zbT, 0, 0, "s")
+            prep_z(3, zbT, 0, 1, "v")
+            wabs[0] = prep_wab(0, abs_[0])
+            bankr = ps_tp.tile([P, 2, P], BF16, name="tpr", tag="tp")
+            for gi in range(2):
+                nc.tensor.transpose(bankr[:, gi, :], Rw[:, gi, :], ident_b[:])
+            nc.vector.tensor_copy(out=cT[:], in_=bankr[:].rearrange("p g c -> p (g c)"))
+            nc.vector.tensor_tensor(out=bsumT[:], in0=cT[:, 128:160], in1=cT[:, 160:192], op=ALU.add)
+            biases[0] = prep_bias(0)
+
+            pend = []
+            done = [0]
+            st = {}
+            hold = {}
+
+            def emit_sq(upto):
+                while done[0] < min(upto, len(pend)):
+                    (seg, acc) = pend[done[0]]
+                    nc.scalar.activation(out=junk[:, 0:CH], in_=seg, func=ACT.Square, accum_out=acc)
+                    done[0] += 1
+
+            def unit(k, bt):
+                half = k // NCH
+                c = k % NCH
+                s = k // 2
+                seg = seg_of(Ut if half == 0 else Vt, bt, c)
+                b0 = bt * P
+                wab = wabs[k]
+                al = ps_al.tile([P, CH], F32, name="al")
+                nc.tensor.matmul(al[:], lhsT=zwT[:, s, b0:b0 + P], rhs=wab[:, 0, :], start=True, stop=True)
+                xh = ps_xh.tile([P, CH], F32, name="xh")
+                for g in range(2):
+                    nc.tensor.matmul_mx(
+                        out=xh[:],
+                        lhsT=xc[half][:, g, b0:b0 + P].bitcast(FP8X4),
+                        lhsT_scale=xs[half][:, g, b0:b0 + P],
+                        rhs=wcs[k][:, g, :].bitcast(FP8X4),
+                        rhs_scale=wss[k][:, g, :],
+                        start=(g == 0),
+                        stop=(g == 1),
+                    )
+                be = ps_be.tile([P, CH], F32, name="be")
+                nc.tensor.matmul(be[:], lhsT=zbT[:, s, b0:b0 + P], rhs=wab[:, 1, :], start=True,
+                                 stop=(half == 0))
+                if half == 1:
+                    nc.tensor.matmul(be[:], lhsT=ident_b[:, c:c + 1].to_broadcast([P, P]), rhs=Bz[:],
+                                     start=False, stop=True)
+                al_sb = alp.tile([P, CH], F32, name="al_sb")
+                nc.scalar.copy(out=al_sb[:], in_=al[:])
+                nc.vector.tensor_tensor(out=seg, in0=xh[:], in1=al_sb[:], op=ALU.mult)
+                nc.vector.scalar_tensor_tensor(out=seg, in0=seg, scalar=1.0, in1=be[:], op0=ALU.mult,
+                                               op1=ALU.add, accum_out=sumU[:, half, bt, c:c + 1])
+                if half == 0:
+                    nc.gpsimd.tensor_tensor(out=seg, in0=seg, in1=biases[c][:], op=ALU.add)
+                pend.append((seg, sqU[:, half, bt, c:c + 1]))
+
+            def fi_item(i):
+                c = i // NB
+                bt = i % NB
+                seg = seg_of(Ut, bt, c)
+                (wbc, bsb) = ficst[c]
+                (mean, rstd) = st["i"]
+                nc.vector.scalar_tensor_tensor(out=seg, in0=seg, scalar=mean[:, bt:bt + 1], in1=wbc[:],
+                                               op0=ALU.subtract, op1=ALU.mult)
+                nc.vector.scalar_tensor_tensor(out=seg, in0=seg, scalar=rstd[:, bt:bt + 1], in1=bsb[:],
+                                               op0=ALU.mult, op1=ALU.add)
+
+            def slot(k, bt):
+                kn = k + 1
+                e4 = ("s", "v", "s", "s") if k < NCH else ("s", "s", "s", "s")
+                if bt == 0 and kn < 2 * NCH:
+                    new_wq(kn)
+                    hold["a"] = mx_half(raws[kn][:], 0, e4[0:2])
+                if bt == 1 and kn < 2 * NCH:
+                    quant(hold["a"], wcs[kn], wss[kn], 0)
+                    hold["b"] = mx_half(raws[kn][:], 1, e4[2:4])
+                    if k + 3 < 2 * NCH:
+                        raws[k + 3] = load_w(k + 3)
+                if bt == 2:
+                    if kn < 2 * NCH:
+                        quant(hold["b"], wcs[kn], wss[kn], 1)
+                        wabs[kn] = prep_wab(kn, abs_[kn // 2])
+                        if kn % 2 == 1 and kn // 2 + 2 < 8:
+                            abs_[kn // 2 + 2] = load_ab(kn // 2 + 2)
+                    if k == 1:
+                        hold["x"] = mx_half(stage_f(1), 0, ("s", "v"))
+                    if k == 2:
+                        hold["x"] = mx_half(stage_f(1), 1, ("s", "v"))
+                    if k == 3:
+                        prep_z(2, zwT, 4, 0, "s")
+                        prep_z(2, zwT, 4, 1, "v")
+                    if k == 4:
+                        prep_z(3, zbT, 4, 0, "s")
+                        prep_z(3, zbT, 4, 1, "v")
+                if bt == 3:
+                    if k == 1:
+                        quant(hold["x"], xc[1], xs[1], 0)
+                    if k == 2:
+                        quant(hold["x"], xc[1], xs[1], 1)
+                    if kn < NCH:
+                        biases[kn] = prep_bias(kn)
+                    elif kn < 2 * NCH:
+                        ficst[kn - NCH] = (prep_w(32, kn - NCH), prep_bsum(kn - NCH))
+
+            for k in range(2 * NCH):
+                for bt in range(NB):
+                    n = k * NB + bt
+                    unit(k, bt)
+                    if n == NB * NCH:
+                        emit_sq(n)
+                        nc.vector.tensor_reduce(out=btot[:], in_=bsm[:], axis=AX.X, op=ALU.add)
+                        st["i"] = half_stats("i", 0, btot[:, 0:1])
+                    else:
+                        emit_sq(n - LAG + 1)
+                    if n > NB * NCH:
+                        fi_item(n - NB * NCH - 1)
+                    slot(k, bt)
+
+            emit_sq(len(pend))
+            order = (4, 5, 0, 1, 2, 3, 6, 7)
+            whs = {}
+            whs[order[0]] = prep_w(64, order[0])
+            fi_item(NB * NCH - 1)
+            st["h"] = half_stats("h", 1, None)
+            whs[order[1]] = prep_w(64, order[1])
+
+            def fh_block(i):
+                c = order[i]
+                (mean, rstd) = st["h"]
+                for bt in range(NB):
+                    vseg = seg_of(Vt, bt, c)
+                    useg = seg_of(Ut, bt, c)
+                    nc.vector.scalar_tensor_tensor(out=vseg, in0=vseg, scalar=mean[:, bt:bt + 1],
+                                                   in1=whs[c][:], op0=ALU.subtract, op1=ALU.mult)
+                    nc.vector.scalar_tensor_tensor(out=useg, in0=vseg, scalar=rstd[:, bt:bt + 1],
+                                                   in1=useg, op0=ALU.mult, op1=ALU.add)
+                if i + 2 < len(order):
+                    whs[order[i + 2]] = prep_w(64, order[i + 2])
+
+            def ureg(bt, q):
+                return Ut[:, bt * NCOL + q * H:bt * NCOL + (q + 1) * H]
+
+            def act_all(q, func):
+                for bt in range(NB):
+                    nc.scalar.activation(out=ureg(bt, q), in_=ureg(bt, q), func=func)
+
+            fh_block(0)
+            fh_block(1)
+            act_all(2, ACT.Sigmoid)
+
+        with tc.tile_pool(name="tailp", bufs=1) as tailp:
+            cxt = tailp.tile([P, NB, H], BF16, name="cxt")
+            nc.sync.dma_start(out=cxt[:], in_=cx.rearrange("(r p) h -> p r h", p=P))
+            wcb = tailp.tile([P, H], BF16, name="wcb")
+            bcb = tailp.tile([P, H], BF16, name="bcb")
+            bankw = bc_bf(96, 8)
+            nc.scalar.copy(out=wcb[:], in_=bankw[:].rearrange("p j c -> p (j c)"))
+            bankb = bc_bf(104, 8)
+            nc.scalar.copy(out=bcb[:], in_=bankb[:].rearrange("p j c -> p (j c)"))
+
+            fh_block(2)
+            fh_block(3)
+            act_all(0, ACT.Sigmoid)
+            for bt in range(NB):
+                nc.vector.tensor_tensor(out=ureg(bt, 2), in0=ureg(bt, 2), in1=cxt[:, bt, :], op=ALU.mult)
+            fh_block(4)
+            fh_block(5)
+            act_all(1, ACT.Tanh)
+            fh_block(6)
+            for bt in range(NB):
+                nc.vector.tensor_tensor(out=ureg(bt, 0), in0=ureg(bt, 0), in1=ureg(bt, 1), op=ALU.mult)
+                nc.vector.scalar_tensor_tensor(out=ureg(bt, 1), in0=ureg(bt, 0), scalar=1.0, in1=ureg(bt, 2),
+                                               op0=ALU.mult, op1=ALU.add, accum_out=sumC[:, bt:bt + 1])
+                nc.scalar.activation(out=junk[:], in_=ureg(bt, 1), func=ACT.Square,
+                                     accum_out=sqC[:, bt:bt + 1])
+            fh_block(7)
+            act_all(3, ACT.Sigmoid)
+            (mean_c, rstd_c) = finish_stats("c", sumC[:], sqC[:], 1.0 / H, None)
+            for bt in range(NB):
+                nc.vector.scalar_tensor_tensor(out=ureg(bt, 1), in0=ureg(bt, 1), scalar=mean_c[:, bt:bt + 1],
+                                               in1=wcb[:], op0=ALU.subtract, op1=ALU.mult)
+                nc.vector.scalar_tensor_tensor(out=ureg(bt, 2), in0=ureg(bt, 1), scalar=rstd_c[:, bt:bt + 1],
+                                               in1=bcb[:], op0=ALU.mult, op1=ALU.add)
+                nc.sync.dma_start(out=out_1[bt * P:(bt + 1) * P, :], in_=ureg(bt, 2))
+                nc.scalar.activation(out=ureg(bt, 0), in_=ureg(bt, 2), func=ACT.Tanh)
+                nc.vector.tensor_tensor(out=ureg(bt, 3), in0=ureg(bt, 3), in1=ureg(bt, 0), op=ALU.mult)
+                nc.sync.dma_start(out=out_0[bt * P:(bt + 1) * P, :], in_=ureg(bt, 3))

@@ -22,7 +22,7 @@ CH = 512
 NCH = NCOL // CH
 EPS = 1e-5
 LAG = 2
-PIN = False
+PIN = True
 
 FLOPS = 2 * 2 * B * NCOL * K + 16 * 2 * B * H * 128
 

@@ -21,8 +21,12 @@ NCOL = 4 * H
 CH = 512
 NCH = NCOL // CH
 EPS = 1e-5
-LAG = 2
+LAG = 3
 PIN = True
+EV_A = ("s", "v", "s", "s")
+EV_B = ("s", "s", "s", "s")
+EV_X = ("s", "v", "s", "v")
+EV_Z = ("s", "v")
 
 FLOPS = 2 * 2 * B * NCOL * K + 16 * 2 * B * H * 128
 
@@ -37,10 +41,6 @@ def tile_adaptivelstmcell_pb_kernel(
             ctx.enter_context(tc.manual_schedule())
         keep = ctx.enter_context(tc.tile_pool(name="keep", bufs=1))
         cst = ctx.enter_context(tc.tile_pool(name="cst", bufs=2))
-        ps_tp = ctx.enter_context(tc.psum_pool(name="ps_tp", bufs=2))
-        ps_xh = ctx.enter_context(tc.psum_pool(name="ps_xh", bufs=2))
-        ps_al = ctx.enter_context(tc.psum_pool(name="ps_al", bufs=2))
-        ps_be = ctx.enter_context(tc.psum_pool(name="ps_be", bufs=2))
 
         Ut = keep.tile([P, NB * NCOL], F32, name="Ut")
         Vt = keep.tile([P, NB * NCOL], F32, name="Vt")
@@ -53,6 +53,7 @@ def tile_adaptivelstmcell_pb_kernel(
         Bz = keep.tile([P, CH], BF16, name="Bz")
         Rw = keep.tile([P, 2, P], BF16, name="Rw")
         cT = keep.tile([P, 2 * P], BF16, name="cT")
+        cTf = keep.tile([P, 2 * P], F32, name="cTf")
         bsumT = keep.tile([P, 32], F32, name="bsumT")
         neghalf = keep.tile([P, NB], F32, name="neghalf")
         dmy = keep.tile([P, 1], F32, name="dmy")
@@ -60,9 +61,13 @@ def tile_adaptivelstmcell_pb_kernel(
         sqU = keep.tile([P, 2, NB, NCH], F32, name="sqU")
         bsm = keep.tile([P, NCH], F32, name="bsm")
         btot = keep.tile([P, 1], F32, name="btot")
-        sumC = keep.tile([P, NB], F32, name="sumC")
-        sqC = keep.tile([P, NB], F32, name="sqC")
+        sumC = keep.tile([P, NB, 2], F32, name="sumC")
+        sqC = keep.tile([P, NB, 2], F32, name="sqC")
         junk = keep.tile([P, H], BF16, name="junk")
+
+        vq = []
+        vqd = [0]
+        st = {}
 
         def copy_on(eng, out, in_):
             if eng == "s":
@@ -87,7 +92,11 @@ def tile_adaptivelstmcell_pb_kernel(
         make_identity(nc, ident_b[:])
 
         with ExitStack() as sctx:
-            rawp = sctx.enter_context(tc.tile_pool(name="rawp", bufs=2))
+            ps_tp = sctx.enter_context(tc.psum_pool(name="ps_tp", bufs=2))
+            ps_xh = sctx.enter_context(tc.psum_pool(name="ps_xh", bufs=2))
+            ps_al = sctx.enter_context(tc.psum_pool(name="ps_al", bufs=2))
+            ps_be = sctx.enter_context(tc.psum_pool(name="ps_be", bufs=2))
+            rawp = sctx.enter_context(tc.tile_pool(name="rawp", bufs=3))
             abp = sctx.enter_context(tc.tile_pool(name="abp", bufs=2))
             grpp = sctx.enter_context(tc.tile_pool(name="grpp", bufs=3))
             wqp = sctx.enter_context(tc.tile_pool(name="wqp", bufs=2))
@@ -163,7 +172,7 @@ def tile_adaptivelstmcell_pb_kernel(
 
             def prep_w(col0, c):
                 bank = bc_bf(col0 + 4 * c, 4)
-                t = cst.tile([P, CH], BF16, name="wbc")
+                t = cst.tile([P, CH], BF16, name="wbc", bufs=3)
                 nc.scalar.copy(out=t[:], in_=bank[:].rearrange("p j c -> p (j c)"))
                 return t
 
@@ -172,46 +181,72 @@ def tile_adaptivelstmcell_pb_kernel(
                 for j in range(4):
                     nc.tensor.transpose(bank[:, j, :],
                                         bsumT[:, 4 * c + j:4 * c + j + 1].to_broadcast([P, P]), ident_f[:])
-                t = cst.tile([P, CH], F32, name="bsb")
+                t = cst.tile([P, CH], F32, name="bsb", bufs=3)
                 nc.scalar.copy(out=t[:], in_=bank[:].rearrange("p j c -> p (j c)"))
                 return t
 
-            def finish_stats(nm, s1, s2, inv_n, shift):
+            def stats_tail(nm, s1, s2, inv_n, shift):
                 mean = keep.tile([P, NB], F32, name="mean_" + nm)
                 msq = keep.tile([P, NB], F32, name="msq_" + nm)
                 var = keep.tile([P, NB], F32, name="var_" + nm)
                 rstd = keep.tile([P, NB], F32, name="rstd_" + nm)
-                if shift is None:
-                    nc.vector.tensor_scalar(out=mean[:], in0=s1, scalar1=inv_n, scalar2=None, op0=ALU.mult)
-                else:
-                    nc.vector.tensor_scalar(out=mean[:], in0=s1, scalar1=shift, scalar2=inv_n,
-                                            op0=ALU.add, op1=ALU.mult)
-                nc.vector.tensor_tensor(out=msq[:], in0=mean[:], in1=mean[:], op=ALU.mult)
-                nc.vector.scalar_tensor_tensor(out=var[:], in0=s2, scalar=inv_n, in1=msq[:],
-                                               op0=ALU.mult, op1=ALU.subtract)
-                nc.vector.tensor_scalar(out=var[:], in0=var[:], scalar1=0.0, scalar2=EPS,
-                                        op0=ALU.max, op1=ALU.add)
-                nc.gpsimd.tensor_tensor(out=rstd[:], in0=var[:], in1=neghalf[:], op=ALU.pow)
-                return (mean, rstd)
+                st[nm] = (mean, rstd)
 
-            def half_stats(nm, half, shift):
+                def j_mean():
+                    if shift is None:
+                        nc.vector.tensor_scalar(out=mean[:], in0=s1, scalar1=inv_n, scalar2=None, op0=ALU.mult)
+                    else:
+                        nc.vector.tensor_scalar(out=mean[:], in0=s1, scalar1=shift, scalar2=inv_n,
+                                                op0=ALU.add, op1=ALU.mult)
+
+                def j_msq():
+                    nc.vector.tensor_tensor(out=msq[:], in0=mean[:], in1=mean[:], op=ALU.mult)
+
+                def j_var():
+                    nc.vector.scalar_tensor_tensor(out=var[:], in0=s2, scalar=inv_n, in1=msq[:],
+                                                   op0=ALU.mult, op1=ALU.subtract)
+
+                def j_rstd():
+                    nc.vector.tensor_scalar(out=var[:], in0=var[:], scalar1=0.0, scalar2=EPS,
+                                            op0=ALU.max, op1=ALU.add)
+                    nc.gpsimd.tensor_tensor(out=rstd[:], in0=var[:], in1=neghalf[:], op=ALU.pow)
+
+                vq.extend([j_mean, j_msq, j_var, j_rstd])
+
+            def stats_jobs(nm, half, with_shift):
                 s1 = keep.tile([P, NB], F32, name="s1_" + nm)
                 s2 = keep.tile([P, NB], F32, name="s2_" + nm)
-                nc.vector.tensor_reduce(out=s1[:], in_=sumU[:, half, :, :], axis=AX.X, op=ALU.add)
-                nc.vector.tensor_reduce(out=s2[:], in_=sqU[:, half, :, :], axis=AX.X, op=ALU.add)
-                return finish_stats(nm, s1[:], s2[:], 1.0 / NCOL, shift)
+
+                def j_s1():
+                    nc.vector.tensor_reduce(out=s1[:], in_=sumU[:, half, :, :], axis=AX.X, op=ALU.add)
+
+                def j_s2():
+                    nc.vector.tensor_reduce(out=s2[:], in_=sqU[:, half, :, :], axis=AX.X, op=ALU.add)
+
+                def j_bt():
+                    nc.vector.tensor_reduce(out=btot[:], in_=bsm[:], axis=AX.X, op=ALU.add)
+
+                vq.extend([j_s1, j_s2])
+                if with_shift:
+                    vq.append(j_bt)
+                stats_tail(nm, s1[:], s2[:], 1.0 / NCOL, btot[:, 0:1] if with_shift else None)
 
             def seg_of(T, bt, c):
                 return T[:, bt * NCOL + c * CH:bt * NCOL + (c + 1) * CH]
 
             zw2 = rows4(zw.rearrange("b s a -> b (s a)"))
             zb2 = rows4(zb.rearrange("b s a -> b (s a)"))
+
+            def stage_z(i, hf):
+                return Vt[:, 4096 + (2 * i + hf) * 1024:4096 + (2 * i + hf + 1) * 1024].bitcast(BF16).rearrange(
+                    "p (r k) -> p r k", r=4)
+
             raws = {}
             abs_ = {}
             nc.sync.dma_start(out=stage_b(0), in_=rows4(x))
             raws[0] = load_w(0)
-            nc.sync.dma_start(out=stage_b(2)[:, :, 0:512], in_=zw2[:, :, 0:512])
-            nc.sync.dma_start(out=stage_b(3)[:, :, 0:512], in_=zb2[:, :, 0:512])
+            nc.sync.dma_start(out=stage_z(0, 0), in_=zw2[:, :, 0:512])
+            nc.sync.dma_start(out=stage_z(1, 0), in_=zb2[:, :, 0:512])
             abs_[0] = load_ab(0)
             for (gi, r0, vec) in ((0, 0, b_ih), (0, 32, ln_i_w), (0, 64, ln_h_w), (0, 96, ln_c_w),
                                   (0, 104, ln_c_b), (1, 0, ln_i_b), (1, 32, ln_h_b)):
@@ -220,46 +255,125 @@ def tile_adaptivelstmcell_pb_kernel(
             nc.sync.dma_start(out=Bz[0:NCH, :], in_=b_hh.rearrange("(c n) -> c n", c=NCH))
             raws[1] = load_w(1)
             abs_[1] = load_ab(1)
+            raws[2] = load_w(2)
             nc.sync.dma_start(out=stage_b(1), in_=rows4(hx))
-            nc.sync.dma_start(out=stage_b(2)[:, :, 512:1024], in_=zw2[:, :, 512:1024])
-            nc.sync.dma_start(out=stage_b(3)[:, :, 512:1024], in_=zb2[:, :, 512:1024])
+            nc.sync.dma_start(out=stage_z(0, 1), in_=zw2[:, :, 512:1024])
+            nc.sync.dma_start(out=stage_z(1, 1), in_=zb2[:, :, 512:1024])
 
             wcs = {}
             wss = {}
             wabs = {}
             biases = {}
             ficst = {}
+            grps = {}
+            evq = []
+            evdone = [0]
+
+            def flush_ev():
+                while evdone[0] < len(evq):
+                    (eng, out, in_, acc) = evq[evdone[0]]
+                    if acc is not None:
+                        nc.scalar.activation(out=out, in_=in_, func=ACT.Copy, accum_out=acc)
+                    else:
+                        copy_on(eng, out, in_)
+                    evdone[0] += 1
 
             def new_wq(k):
                 wcs[k] = wqp.tile([P, 2, CH], U32, name="wc", align_bytes=64)
                 wss[k] = wqp.tile([P, 2, CH], U8, name="ws", align_bytes=64)
 
-            g0 = mx_half(stage_f(0), 0, ("s", "v"))
-            g1 = mx_half(stage_f(0), 1, ("s", "v"))
-            quant(g0, xc[0], xs[0], 0)
+            def t_words(key, src, j, eng):
+                g = j // 2
+                rp = j % 2
+                if rp == 0:
+                    grps[(key, g)] = grpp.tile([P, 2048], BF16, name="grp", align_bytes=64)
+                gview = grps[(key, g)][:].bitcast(F32).rearrange("p (n u) -> p n u", u=2)
+                bank = ps_tp.tile([P, 2, 2, P], F32, name="tpw", tag="tp")
+                for u in range(2):
+                    for r2 in range(2):
+                        col = (2 * rp + r2) * 512 + 256 * g + 128 * u
+                        nc.tensor.transpose(bank[:, u, r2, :], src[:, col:col + P], ident_f[:])
+                evq.append((eng, gview[:, 256 * rp:256 * rp + 256, :],
+                            bank[:].rearrange("p u r c -> p (r c) u"), None))
+
+            def t_z(i, hf, dstT, bp, eng):
+                srcb = stage_z(i, hf)
+                bank = ps_tp.tile([P, 4, 2, P], BF16, name="tpz", tag="tp")
+                for s in range(4):
+                    for bl in range(2):
+                        nc.tensor.transpose(bank[:, s, bl, :], srcb[:, 2 * bp + bl, s * P:(s + 1) * P], ident_b[:])
+                evq.append((eng, dstT[:, 4 * hf:4 * hf + 4, 256 * bp:256 * bp + 256],
+                            bank[:].rearrange("p s l b -> p s (l b)"), None))
+
+            def t_wab(k):
+                ab = abs_[k // 2]
+                hh = k % 2
+                bank = ps_tp.tile([P, 2, 4, P], BF16, name="tpab", tag="tp")
+                for j in range(2):
+                    for r in range(4):
+                        nc.tensor.transpose(bank[:, j, r, :], ab[j][:, hh * 4 + r, :], ident_b[:])
+                wabs[k] = wabp.tile([P, 2, CH], BF16, name="wab")
+                evq.append(("s", wabs[k][:], bank[:].rearrange("p j r c -> p j (r c)"), None))
+
+            def t_bias(c):
+                bank = bc_bf(4 * c, 4)
+                biases[c] = cst.tile([P, CH], BF16, name="biasbc")
+                evq.append(("s", biases[c][:], bank[:].rearrange("p j c -> p (j c)"), bsm[:, c:c + 1]))
+
+            def t_w(col0, c, store):
+                bank = bc_bf(col0 + 4 * c, 4)
+                store[c] = cst.tile([P, CH], BF16, name="wbc", bufs=3)
+                evq.append(("s", store[c][:], bank[:].rearrange("p j c -> p (j c)"), None))
+
+            def t_bsum(c, store):
+                bank = ps_tp.tile([P, 4, P], F32, name="tpf", tag="tp")
+                for j in range(4):
+                    nc.tensor.transpose(bank[:, j, :],
+                                        bsumT[:, 4 * c + j:4 * c + j + 1].to_broadcast([P, P]), ident_f[:])
+                store[c] = cst.tile([P, CH], F32, name="bsb", bufs=3)
+                evq.append(("s", store[c][:], bank[:].rearrange("p j c -> p (j c)"), None))
+
+            def quant_key(key, g, codes, scales):
+                quant(grps[(key, g)], codes, scales, g)
+
+            for j in range(4):
+                t_words("x", stage_f(0), j, "sv"[j % 2])
+                if j % 2 == 1:
+                    flush_ev()
+            quant_key("x", 0, xc[0], xs[0])
             new_wq(0)
-            g2 = mx_half(raws[0][:], 0, ("s", "v"))
-            quant(g1, xc[0], xs[0], 1)
-            g3 = mx_half(raws[0][:], 1, ("s", "v"))
-            quant(g2, wcs[0], wss[0], 0)
-            raws[2] = load_w(2)
-            prep_z(2, zwT, 0, 0, "s")
-            prep_z(2, zwT, 0, 1, "v")
-            quant(g3, wcs[0], wss[0], 1)
-            prep_z(3, zbT, 0, 0, "s")
-            prep_z(3, zbT, 0, 1, "v")
-            wabs[0] = prep_wab(0, abs_[0])
+            t_words(0, raws[0][:], 0, "s")
+            t_words(0, raws[0][:], 1, "v")
+            flush_ev()
+            quant_key("x", 1, xc[0], xs[0])
+            t_words(0, raws[0][:], 2, "s")
+            t_words(0, raws[0][:], 3, "v")
+            flush_ev()
+            quant_key(0, 0, wcs[0], wss[0])
+            raws[3] = load_w(3)
+            t_z(0, 0, zwT, 0, "s")
+            t_z(0, 0, zwT, 1, "v")
+            flush_ev()
+            quant_key(0, 1, wcs[0], wss[0])
+            t_z(1, 0, zbT, 0, "s")
+            t_z(1, 0, zbT, 1, "v")
+            flush_ev()
             bankr = ps_tp.tile([P, 2, P], BF16, name="tpr", tag="tp")
             for gi in range(2):
                 nc.tensor.transpose(bankr[:, gi, :], Rw[:, gi, :], ident_b[:])
             nc.vector.tensor_copy(out=cT[:], in_=bankr[:].rearrange("p g c -> p (g c)"))
             nc.vector.tensor_tensor(out=bsumT[:], in0=cT[:, 128:160], in1=cT[:, 160:192], op=ALU.add)
-            biases[0] = prep_bias(0)
+            nc.vector.tensor_copy(out=cTf[:], in_=cT[:])
 
             pend = []
             done = [0]
-            st = {}
-            hold = {}
+            als = {}
+            alsb = {}
+            fiw = {}
+            fib = {}
+            NU = 2 * NCH * NB
+            extras = [("x", 0), ("x", 1), ("x", 2), ("x", 3), ("z", 0, 0), ("z", 0, 1), ("z", 1, 0), ("z", 1, 1)]
+            exdone = [0]
 
             def emit_sq(upto):
                 while done[0] < min(upto, len(pend)):
@@ -267,15 +381,114 @@ def tile_adaptivelstmcell_pb_kernel(
                     nc.scalar.activation(out=junk[:, 0:CH], in_=seg, func=ACT.Square, accum_out=acc)
                     done[0] += 1
 
-            def unit(k, bt):
+            def pe_al(n):
+                k = n // NB
+                b0 = (n % NB) * P
+                als[n] = ps_al.tile([P, CH], F32, name="al")
+                nc.tensor.matmul(als[n][:], lhsT=zwT[:, k // 2, b0:b0 + P], rhs=wabs[k][:, 0, :], start=True, stop=True)
+
+            def s_al(n):
+                alsb[n] = alp.tile([P, CH], F32, name="al_sb")
+                nc.scalar.copy(out=alsb[n][:], in_=als[n][:])
+
+            def extra_job():
+                if exdone[0] < len(extras):
+                    e = extras[exdone[0]]
+                    if e[0] == "x":
+                        t_words("h", stage_f(1), e[1], EV_X[e[1]])
+                    else:
+                        t_z(e[1], 1, zwT if e[1] == 0 else zbT, e[2], EV_Z[e[2]])
+                    exdone[0] += 1
+
+            def pe_slot(n):
+                k = n // NB
+                r = n % NB
+                ev = EV_A if n < NB * NCH - 4 else EV_B
+                if n == 0:
+                    t_words(1, raws[1][:], 0, "s")
+                    t_words(1, raws[1][:], 1, "v")
+                elif n == 1:
+                    t_words(1, raws[1][:], 2, "s")
+                    t_words(1, raws[1][:], 3, "v")
+                    raws[4] = load_w(4)
+                elif n == 2:
+                    t_words(2, raws[2][:], 0, "s")
+                    t_words(2, raws[2][:], 1, "v")
+                elif r == 0:
+                    if k + 1 < 2 * NCH:
+                        t_words(k + 1, raws[k + 1][:], 3, ev[3])
+                        if k + 4 < 2 * NCH:
+                            raws[k + 4] = load_w(k + 4)
+                    if 1 <= k <= 4:
+                        extra_job()
+                else:
+                    if k + 2 < 2 * NCH:
+                        t_words(k + 2, raws[k + 2][:], r - 1, ev[r - 1])
+                if r == 1 and k + 1 < 2 * NCH:
+                    t_wab(k + 1)
+                    if (k + 1) % 2 == 1 and (k + 1) // 2 + 2 < 8:
+                        abs_[(k + 1) // 2 + 2] = load_ab((k + 1) // 2 + 2)
+                if r == 2:
+                    if k + 1 < NCH:
+                        t_bias(k + 1)
+
+                if r == 3:
+                    if 1 <= k <= 4:
+                        extra_job()
+
+
+            def v_quants(n):
+                k = n // NB
+                r = n % NB
+                if k == 0:
+                    if r == 2:
+                        new_wq(1)
+                        quant_key(1, 0, wcs[1], wss[1])
+                    if r == 3:
+                        quant_key(1, 1, wcs[1], wss[1])
+                elif r == 0 and k + 1 < 2 * NCH:
+                    new_wq(k + 1)
+                    quant_key(k + 1, 0, wcs[k + 1], wss[k + 1])
+                elif r == 2 and k + 1 < 2 * NCH:
+                    quant_key(k + 1, 1, wcs[k + 1], wss[k + 1])
+                if r == 1 and k == 2:
+                    quant_key("h", 0, xc[1], xs[1])
+                if r == 1 and k == 3:
+                    quant_key("h", 1, xc[1], xs[1])
+
+            def g_norm(i):
+                bt = i % NB
+                o = bt * NCOL + (i // NB) * H
+                nc.vector.tensor_scalar(out=Ut[:, o:o + H], in0=Ut[:, o:o + H], scalar1=st["i"][0][:, bt:bt + 1],
+                                        scalar2=st["i"][1][:, bt:bt + 1], op0=ALU.subtract, op1=ALU.mult)
+
+            def drip(m):
+                for t in range(m):
+                    if vqd[0] < len(vq):
+                        vq[vqd[0]]()
+                        vqd[0] += 1
+
+            bes = {}
+            segs = {}
+            fid = [0]
+            FI0 = NB * NCH + 3
+
+            def v_c(n):
+                k = n // NB
+                half = k // NCH
+                nc.vector.scalar_tensor_tensor(out=segs[n], in0=segs[n], scalar=1.0, in1=bes[n][:], op0=ALU.mult,
+                                               op1=ALU.add, accum_out=sumU[:, half, n % NB, k % NCH:k % NCH + 1])
+                if half == 0:
+                    nc.gpsimd.tensor_tensor(out=segs[n], in0=segs[n], in1=biases[k][:], op=ALU.add)
+                pend.append((segs[n], sqU[:, half, n % NB, k % NCH:k % NCH + 1]))
+
+            def step(n):
+                k = n // NB
+                bt = n % NB
                 half = k // NCH
                 c = k % NCH
-                s = k // 2
-                seg = seg_of(Ut if half == 0 else Vt, bt, c)
+                segs[n] = seg_of(Ut if half == 0 else Vt, bt, c)
                 b0 = bt * P
-                wab = wabs[k]
-                al = ps_al.tile([P, CH], F32, name="al")
-                nc.tensor.matmul(al[:], lhsT=zwT[:, s, b0:b0 + P], rhs=wab[:, 0, :], start=True, stop=True)
                 xh = ps_xh.tile([P, CH], F32, name="xh")
                 for g in range(2):
                     nc.tensor.matmul_mx(
@@ -287,149 +500,226 @@ def tile_adaptivelstmcell_pb_kernel(
                         start=(g == 0),
                         stop=(g == 1),
                     )
-                be = ps_be.tile([P, CH], F32, name="be")
-                nc.tensor.matmul(be[:], lhsT=zbT[:, s, b0:b0 + P], rhs=wab[:, 1, :], start=True,
+                flush_ev()
+                if n + 1 < NU:
+                    pe_al(n + 1)
+                    s_al(n + 1)
+                pe_slot(n)
+                bes[n] = ps_be.tile([P, CH], F32, name="be")
+                nc.tensor.matmul(bes[n][:], lhsT=zbT[:, k // 2, b0:b0 + P], rhs=wabs[k][:, 1, :], start=True,
                                  stop=(half == 0))
                 if half == 1:
-                    nc.tensor.matmul(be[:], lhsT=ident_b[:, c:c + 1].to_broadcast([P, P]), rhs=Bz[:],
+                    nc.tensor.matmul(bes[n][:], lhsT=ident_b[:, c:c + 1].to_broadcast([P, P]), rhs=Bz[:],
                                      start=False, stop=True)
-                al_sb = alp.tile([P, CH], F32, name="al_sb")
-                nc.scalar.copy(out=al_sb[:], in_=al[:])
-                nc.vector.tensor_tensor(out=seg, in0=xh[:], in1=al_sb[:], op=ALU.mult)
-                nc.vector.scalar_tensor_tensor(out=seg, in0=seg, scalar=1.0, in1=be[:], op0=ALU.mult,
-                                               op1=ALU.add, accum_out=sumU[:, half, bt, c:c + 1])
-                if half == 0:
-                    nc.gpsimd.tensor_tensor(out=seg, in0=seg, in1=biases[c][:], op=ALU.add)
-                pend.append((seg, sqU[:, half, bt, c:c + 1]))
+                emit_sq(n - LAG + 1)
+                v_quants(n)
+                nc.vector.tensor_tensor(out=segs[n], in0=xh[:], in1=alsb[n][:], op=ALU.mult)
+                if n >= FI0 + 4 and fid[0] < 4 * NB:
+                    g_norm(fid[0])
+                    fid[0] += 1
+                else:
+                    drip(1)
+                if n > 0:
+                    v_c(n - 1)
+                drip(1)
+                if n == FI0 - 1:
+                    emit_sq(NB * NCH)
+                    stats_jobs("i", 0, True)
 
-            def fi_item(i):
-                c = i // NB
-                bt = i % NB
-                seg = seg_of(Ut, bt, c)
-                (wbc, bsb) = ficst[c]
-                (mean, rstd) = st["i"]
-                nc.vector.scalar_tensor_tensor(out=seg, in0=seg, scalar=mean[:, bt:bt + 1], in1=wbc[:],
-                                               op0=ALU.subtract, op1=ALU.mult)
-                nc.vector.scalar_tensor_tensor(out=seg, in0=seg, scalar=rstd[:, bt:bt + 1], in1=bsb[:],
-                                               op0=ALU.mult, op1=ALU.add)
-
-            def slot(k, bt):
-                kn = k + 1
-                e4 = ("s", "v", "s", "s") if k < NCH else ("s", "s", "s", "s")
-                if bt == 0 and kn < 2 * NCH:
-                    new_wq(kn)
-                    hold["a"] = mx_half(raws[kn][:], 0, e4[0:2])
-                if bt == 1 and kn < 2 * NCH:
-                    quant(hold["a"], wcs[kn], wss[kn], 0)
-                    hold["b"] = mx_half(raws[kn][:], 1, e4[2:4])
-                    if k + 3 < 2 * NCH:
-                        raws[k + 3] = load_w(k + 3)
-                if bt == 2:
-                    if kn < 2 * NCH:
-                        quant(hold["b"], wcs[kn], wss[kn], 1)
-                        wabs[kn] = prep_wab(kn, abs_[kn // 2])
-                        if kn % 2 == 1 and kn // 2 + 2 < 8:
-                            abs_[kn // 2 + 2] = load_ab(kn // 2 + 2)
-                    if k == 1:
-                        hold["x"] = mx_half(stage_f(1), 0, ("s", "v"))
-                    if k == 2:
-                        hold["x"] = mx_half(stage_f(1), 1, ("s", "v"))
-                    if k == 3:
-                        prep_z(2, zwT, 4, 0, "s")
-                        prep_z(2, zwT, 4, 1, "v")
-                    if k == 4:
-                        prep_z(3, zbT, 4, 0, "s")
-                        prep_z(3, zbT, 4, 1, "v")
-                if bt == 3:
-                    if k == 1:
-                        quant(hold["x"], xc[1], xs[1], 0)
-                    if k == 2:
-                        quant(hold["x"], xc[1], xs[1], 1)
-                    if kn < NCH:
-                        biases[kn] = prep_bias(kn)
-                    elif kn < 2 * NCH:
-                        ficst[kn - NCH] = (prep_w(32, kn - NCH), prep_bsum(kn - NCH))
-
-            for k in range(2 * NCH):
-                for bt in range(NB):
-                    n = k * NB + bt
-                    unit(k, bt)
-                    if n == NB * NCH:
-                        emit_sq(n)
-                        nc.vector.tensor_reduce(out=btot[:], in_=bsm[:], axis=AX.X, op=ALU.add)
-                        st["i"] = half_stats("i", 0, btot[:, 0:1])
-                    else:
-                        emit_sq(n - LAG + 1)
-                    if n > NB * NCH:
-                        fi_item(n - NB * NCH - 1)
-                    slot(k, bt)
+            t_wab(0)
+            t_bias(0)
+            flush_ev()
+            pe_al(0)
+            s_al(0)
+            for n in range(NU):
+                step(n)
+            v_c(NU - 1)
 
             emit_sq(len(pend))
-            order = (4, 5, 0, 1, 2, 3, 6, 7)
-            whs = {}
-            whs[order[0]] = prep_w(64, order[0])
-            fi_item(NB * NCH - 1)
-            st["h"] = half_stats("h", 1, None)
-            whs[order[1]] = prep_w(64, order[1])
+            stats_jobs("h", 1, False)
+            drip(16)
 
-            def fh_block(i):
-                c = order[i]
-                (mean, rstd) = st["h"]
-                for bt in range(NB):
-                    vseg = seg_of(Vt, bt, c)
-                    useg = seg_of(Ut, bt, c)
-                    nc.vector.scalar_tensor_tensor(out=vseg, in0=vseg, scalar=mean[:, bt:bt + 1],
-                                                   in1=whs[c][:], op0=ALU.subtract, op1=ALU.mult)
-                    nc.vector.scalar_tensor_tensor(out=useg, in0=vseg, scalar=rstd[:, bt:bt + 1],
-                                                   in1=useg, op0=ALU.mult, op1=ALU.add)
-                if i + 2 < len(order):
-                    whs[order[i + 2]] = prep_w(64, order[i + 2])
-
-            def ureg(bt, q):
-                return Ut[:, bt * NCOL + q * H:bt * NCOL + (q + 1) * H]
-
-            def act_all(q, func):
-                for bt in range(NB):
-                    nc.scalar.activation(out=ureg(bt, q), in_=ureg(bt, q), func=func)
-
-            fh_block(0)
-            fh_block(1)
-            act_all(2, ACT.Sigmoid)
-
-        with tc.tile_pool(name="tailp", bufs=1) as tailp:
-            cxt = tailp.tile([P, NB, H], BF16, name="cxt")
-            nc.sync.dma_start(out=cxt[:], in_=cx.rearrange("(r p) h -> p r h", p=P))
+        with ExitStack() as tctx:
+            tailp = tctx.enter_context(tc.tile_pool(name="tailp", bufs=1))
+            xp = tctx.enter_context(tc.tile_pool(name="xp", bufs=3))
+            gp = tctx.enter_context(tc.tile_pool(name="gp", bufs=2))
+            psA = tctx.enter_context(tc.psum_pool(name="psA", bufs=3))
+            psB = tctx.enter_context(tc.psum_pool(name="psB", bufs=3))
+            psC = tctx.enter_context(tc.psum_pool(name="psC", bufs=2))
+            cxs = tailp.tile([P, NB, H], BF16, name="cxs")
+            nc.sync.dma_start(out=cxs[:], in_=cx.rearrange("(r p) h -> p r h", p=P))
+            cTall = tailp.tile([P, 8, B], F32, name="cTall")
+            soall = tailp.tile([P, 8, B], F32, name="soall")
             wcb = tailp.tile([P, H], BF16, name="wcb")
             bcb = tailp.tile([P, H], BF16, name="bcb")
-            bankw = bc_bf(96, 8)
-            nc.scalar.copy(out=wcb[:], in_=bankw[:].rearrange("p j c -> p (j c)"))
-            bankb = bc_bf(104, 8)
-            nc.scalar.copy(out=bcb[:], in_=bankb[:].rearrange("p j c -> p (j c)"))
+            QORD = (2, 0, 1, 3)
+            NJ = 32
+            aTs = {}
+            bTs = {}
+            Xs = {}
+            gs = {}
+            cxTs = {}
 
-            fh_block(2)
-            fh_block(3)
-            act_all(0, ACT.Sigmoid)
-            for bt in range(NB):
-                nc.vector.tensor_tensor(out=ureg(bt, 2), in0=ureg(bt, 2), in1=cxt[:, bt, :], op=ALU.mult)
-            fh_block(4)
-            fh_block(5)
-            act_all(1, ACT.Tanh)
-            fh_block(6)
-            for bt in range(NB):
-                nc.vector.tensor_tensor(out=ureg(bt, 0), in0=ureg(bt, 0), in1=ureg(bt, 1), op=ALU.mult)
-                nc.vector.scalar_tensor_tensor(out=ureg(bt, 1), in0=ureg(bt, 0), scalar=1.0, in1=ureg(bt, 2),
-                                               op0=ALU.mult, op1=ALU.add, accum_out=sumC[:, bt:bt + 1])
-                nc.scalar.activation(out=junk[:], in_=ureg(bt, 1), func=ACT.Square,
-                                     accum_out=sqC[:, bt:bt + 1])
-            fh_block(7)
-            act_all(3, ACT.Sigmoid)
-            (mean_c, rstd_c) = finish_stats("c", sumC[:], sqC[:], 1.0 / H, None)
-            for bt in range(NB):
-                nc.vector.scalar_tensor_tensor(out=ureg(bt, 1), in0=ureg(bt, 1), scalar=mean_c[:, bt:bt + 1],
-                                               in1=wcb[:], op0=ALU.subtract, op1=ALU.mult)
-                nc.vector.scalar_tensor_tensor(out=ureg(bt, 2), in0=ureg(bt, 1), scalar=rstd_c[:, bt:bt + 1],
-                                               in1=bcb[:], op0=ALU.mult, op1=ALU.add)
-                nc.sync.dma_start(out=out_1[bt * P:(bt + 1) * P, :], in_=ureg(bt, 2))
-                nc.scalar.activation(out=ureg(bt, 0), in_=ureg(bt, 2), func=ACT.Tanh)
-                nc.vector.tensor_tensor(out=ureg(bt, 3), in0=ureg(bt, 3), in1=ureg(bt, 0), op=ALU.mult)
-                nc.sync.dma_start(out=out_0[bt * P:(bt + 1) * P, :], in_=ureg(bt, 3))
+            def hq(j):
+                return (j // 4, QORD[j % 4])
+
+            def n_norm(hb):
+                for bt in range(NB):
+                    ap = Vt[:, bt * NCOL:(bt + 1) * NCOL].rearrange("p (q h) -> p q h", q=4)[:, :, hb * P:(hb + 1) * P]
+                    nc.vector.tensor_scalar(out=ap, in0=ap, scalar1=st["h"][0][:, bt:bt + 1],
+                                            scalar2=st["h"][1][:, bt:bt + 1], op0=ALU.subtract, op1=ALU.mult)
+
+            def t_a(j):
+                (hb, q) = hq(j)
+                aTs[j] = psA.tile([P, NB, P], F32, name="aT")
+                for bt in range(NB):
+                    col = bt * NCOL + q * H + hb * P
+                    nc.tensor.transpose(aTs[j][:, bt, :], Ut[:, col:col + P], ident_f[:])
+
+            def t_b(j):
+                (hb, q) = hq(j)
+                bTs[j] = psB.tile([P, NB, P], F32, name="bT")
+                for bt in range(NB):
+                    col = bt * NCOL + q * H + hb * P
+                    nc.tensor.transpose(bTs[j][:, bt, :], Vt[:, col:col + P], ident_f[:])
+
+            def t_cx(hb):
+                cxTs[hb] = psC.tile([P, NB, P], BF16, name="cxT")
+                for bt in range(NB):
+                    nc.tensor.transpose(cxTs[hb][:, bt, :], cxs[:, bt, hb * P:(hb + 1) * P], ident_b[:])
+
+            def s_x(j):
+                (hb, q) = hq(j)
+                m = q * 8 + hb
+                Xs[j] = xp.tile([P, B], F32, name="X")
+                nc.scalar.activation(out=Xs[j][:], in_=bTs[j][:].rearrange("p b c -> p (b c)"), func=ACT.Identity,
+                                     scale=cTf[:, 64 + m:65 + m], bias=bsumT[:, m:m + 1])
+
+            def v_m(j):
+                (hb, q) = hq(j)
+                m = q * 8 + hb
+                if q == 3:
+                    gs[j] = soall[:, hb, :]
+                else:
+                    gt = gp.tile([P, B], F32, name="g%d" % q)
+                    gs[j] = gt[:]
+                nc.vector.scalar_tensor_tensor(out=gs[j], in0=aTs[j][:].rearrange("p b c -> p (b c)"),
+                                               scalar=cTf[:, 32 + m:33 + m], in1=Xs[j][:], op0=ALU.mult, op1=ALU.add)
+
+            def s_act(j):
+                nc.scalar.activation(out=gs[j], in_=gs[j], func=(ACT.Tanh if hq(j)[1] == 1 else ACT.Sigmoid))
+
+            def v_pq(hb):
+                nc.vector.tensor_tensor(out=gs[4 * hb], in0=gs[4 * hb], in1=cxTs[hb][:].rearrange("p b c -> p (b c)"),
+                                        op=ALU.mult)
+                nc.vector.tensor_tensor(out=gs[4 * hb + 1], in0=gs[4 * hb + 1], in1=gs[4 * hb + 2], op=ALU.mult)
+
+            def v_c2(hb):
+                nc.vector.tensor_tensor(out=cTall[:, hb, :], in0=gs[4 * hb], in1=gs[4 * hb + 1], op=ALU.add)
+
+            def bc_tail(col0, dst):
+                bank = psC.tile([P, 8, P], BF16, name="cxT")
+                for j in range(8):
+                    nc.tensor.transpose(bank[:, j, :], cT[:, col0 + j:col0 + j + 1].to_broadcast([P, P]), ident_b[:])
+                nc.scalar.copy(out=dst, in_=bank[:].rearrange("p j c -> p (j c)"))
+
+            bc_tail(96, wcb[:])
+            bc_tail(104, bcb[:])
+            t_a(0)
+            t_a(1)
+            n_norm(0)
+            for j in range(-2, NJ + 3):
+                if 0 <= j + 2 < NJ:
+                    if (j + 2) % 4 == 0:
+                        t_cx((j + 2) // 4)
+                    if j + 2 >= 2:
+                        t_a(j + 2)
+                    t_b(j + 2)
+                if 0 <= j + 1 < NJ:
+                    s_x(j + 1)
+                if 0 <= j - 1 < NJ:
+                    s_act(j - 1)
+                if 0 <= j < NJ:
+                    v_m(j)
+                    if j % 4 == 0 and j // 4 + 1 < 8:
+                        n_norm(j // 4 + 1)
+                if j >= 5 and (j - 5) % 4 == 0:
+                    v_pq((j - 5) // 4)
+                if j >= 6 and (j - 6) % 4 == 0:
+                    v_c2((j - 6) // 4)
+
+            s1c = keep.tile([P, NB], F32, name="s1c")
+            s2c = keep.tile([P, NB], F32, name="s2c")
+            mec = keep.tile([P, NB], F32, name="mec")
+            msc = keep.tile([P, NB], F32, name="msc")
+            vac = keep.tile([P, NB], F32, name="vac")
+            rsc = keep.tile([P, NB], F32, name="rsc")
+            cbs = {}
+            sbs = {}
+
+            def cyr(bt):
+                return Ut[:, bt * NCOL:bt * NCOL + H]
+
+            def tcr(bt):
+                return Ut[:, bt * NCOL + H:bt * NCOL + 2 * H]
+
+            def e_back(bt, src, pool, nm, store):
+                store[bt] = []
+                for hf in range(2):
+                    t = pool.tile([P, NB, P], F32, name=nm)
+                    store[bt].append(t)
+                    for i in range(4):
+                        nc.tensor.transpose(t[:, i, :], src[:, 4 * hf + i, bt * P:(bt + 1) * P], ident_f[:])
+
+            def flat(t):
+                return t[:].rearrange("p b c -> p (b c)")
+
+            def e_sums(bt):
+                for hf in range(2):
+                    nc.scalar.activation(out=junk[:, 0:CH], in_=flat(cbs[bt][hf]), func=ACT.Copy,
+                                         accum_out=sumC[:, bt, hf:hf + 1])
+                    nc.scalar.activation(out=junk[:, CH:2 * CH], in_=flat(cbs[bt][hf]), func=ACT.Square,
+                                         accum_out=sqC[:, bt, hf:hf + 1])
+
+            def e_stats(bt):
+                c1 = slice(bt, bt + 1)
+                nc.vector.tensor_tensor(out=s1c[:, c1], in0=sumC[:, bt, 0:1], in1=sumC[:, bt, 1:2], op=ALU.add)
+                nc.vector.tensor_tensor(out=s2c[:, c1], in0=sqC[:, bt, 0:1], in1=sqC[:, bt, 1:2], op=ALU.add)
+                nc.vector.tensor_scalar(out=mec[:, c1], in0=s1c[:, c1], scalar1=1.0 / H, scalar2=None, op0=ALU.mult)
+                nc.vector.tensor_tensor(out=msc[:, c1], in0=mec[:, c1], in1=mec[:, c1], op=ALU.mult)
+                nc.vector.scalar_tensor_tensor(out=vac[:, c1], in0=s2c[:, c1], scalar=1.0 / H, in1=msc[:, c1],
+                                               op0=ALU.mult, op1=ALU.subtract)
+                nc.vector.tensor_scalar(out=vac[:, c1], in0=vac[:, c1], scalar1=0.0, scalar2=EPS,
+                                        op0=ALU.max, op1=ALU.add)
+                nc.gpsimd.tensor_tensor(out=rsc[:, c1], in0=vac[:, c1], in1=neghalf[:, c1], op=ALU.pow)
+
+            def e_a(bt):
+                for hf in range(2):
+                    nc.vector.scalar_tensor_tensor(out=cyr(bt)[:, hf * CH:(hf + 1) * CH], in0=flat(cbs[bt][hf]),
+                                                   scalar=mec[:, bt:bt + 1], in1=wcb[:, hf * CH:(hf + 1) * CH],
+                                                   op0=ALU.subtract, op1=ALU.mult)
+
+            def e_cy(bt):
+                nc.vector.scalar_tensor_tensor(out=cyr(bt), in0=cyr(bt), scalar=rsc[:, bt:bt + 1], in1=bcb[:],
+                                               op0=ALU.mult, op1=ALU.add)
+                nc.sync.dma_start(out=out_1[bt * P:(bt + 1) * P, :], in_=cyr(bt))
+                nc.scalar.activation(out=tcr(bt), in_=cyr(bt), func=ACT.Tanh)
+
+            def e_hy(bt):
+                for hf in range(2):
+                    nc.vector.tensor_tensor(out=tcr(bt)[:, hf * CH:(hf + 1) * CH], in0=tcr(bt)[:, hf * CH:(hf + 1) * CH],
+                                            in1=flat(sbs[bt][hf]), op=ALU.mult)
+                nc.sync.dma_start(out=out_0[bt * P:(bt + 1) * P, :], in_=tcr(bt))
+
+            for t in range(NB + 3):
+                if t < NB:
+                    e_back(t, cTall, psA, "aT", cbs)
+                    e_sums(t)
+                if 0 <= t - 1 < NB:
+                    e_stats(t - 1)
+                    e_back(t - 1, soall, psB, "bT", sbs)
+                    e_a(t - 1)
+                if 0 <= t - 3 < NB:
+                    e_hy(t - 3)
+                if 0 <= t - 1 < NB:
+                    e_cy(t - 1)

@@ -27,6 +27,9 @@ EV_A = ("s", "v", "s", "s")
 EV_B = ("s", "s", "s", "s")
 EV_X = ("s", "v", "s", "v")
 EV_Z = ("s", "v")
+GLAST = 7
+WAB_V = ()
+XV = ()
 
 FLOPS = 2 * 2 * B * NCOL * K + 16 * 2 * B * H * 128
 
@@ -248,17 +251,14 @@ def tile_adaptivelstmcell_pb_kernel(
             nc.sync.dma_start(out=stage_z(0, 0), in_=zw2[:, :, 0:512])
             nc.sync.dma_start(out=stage_z(1, 0), in_=zb2[:, :, 0:512])
             abs_[0] = load_ab(0)
+            raws[1] = load_w(1)
             for (gi, r0, vec) in ((0, 0, b_ih), (0, 32, ln_i_w), (0, 64, ln_h_w), (0, 96, ln_c_w),
                                   (0, 104, ln_c_b), (1, 0, ln_i_b), (1, 32, ln_h_b)):
                 m = vec.shape[0] // P
                 nc.sync.dma_start(out=Rw[r0:r0 + m, gi, :], in_=vec.rearrange("(m p) -> m p", p=P))
             nc.sync.dma_start(out=Bz[0:NCH, :], in_=b_hh.rearrange("(c n) -> c n", c=NCH))
-            raws[1] = load_w(1)
             abs_[1] = load_ab(1)
             raws[2] = load_w(2)
-            nc.sync.dma_start(out=stage_b(1), in_=rows4(hx))
-            nc.sync.dma_start(out=stage_z(0, 1), in_=zw2[:, :, 512:1024])
-            nc.sync.dma_start(out=stage_z(1, 1), in_=zb2[:, :, 512:1024])
 
             wcs = {}
             wss = {}
@@ -278,6 +278,10 @@ def tile_adaptivelstmcell_pb_kernel(
                         copy_on(eng, out, in_)
                     evdone[0] += 1
 
+            def room():
+                if len(evq) - evdone[0] >= 2:
+                    flush_ev()
+
             def new_wq(k):
                 wcs[k] = wqp.tile([P, 2, CH], U32, name="wc", align_bytes=64)
                 wss[k] = wqp.tile([P, 2, CH], U8, name="ws", align_bytes=64)
@@ -288,6 +292,7 @@ def tile_adaptivelstmcell_pb_kernel(
                 if rp == 0:
                     grps[(key, g)] = grpp.tile([P, 2048], BF16, name="grp", align_bytes=64)
                 gview = grps[(key, g)][:].bitcast(F32).rearrange("p (n u) -> p n u", u=2)
+                room()
                 bank = ps_tp.tile([P, 2, 2, P], F32, name="tpw", tag="tp")
                 for u in range(2):
                     for r2 in range(2):
@@ -298,6 +303,7 @@ def tile_adaptivelstmcell_pb_kernel(
 
             def t_z(i, hf, dstT, bp, eng):
                 srcb = stage_z(i, hf)
+                room()
                 bank = ps_tp.tile([P, 4, 2, P], BF16, name="tpz", tag="tp")
                 for s in range(4):
                     for bl in range(2):
@@ -308,14 +314,16 @@ def tile_adaptivelstmcell_pb_kernel(
             def t_wab(k):
                 ab = abs_[k // 2]
                 hh = k % 2
+                room()
                 bank = ps_tp.tile([P, 2, 4, P], BF16, name="tpab", tag="tp")
                 for j in range(2):
                     for r in range(4):
                         nc.tensor.transpose(bank[:, j, r, :], ab[j][:, hh * 4 + r, :], ident_b[:])
                 wabs[k] = wabp.tile([P, 2, CH], BF16, name="wab")
-                evq.append(("s", wabs[k][:], bank[:].rearrange("p j r c -> p j (r c)"), None))
+                evq.append(("v" if k in WAB_V else "s", wabs[k][:], bank[:].rearrange("p j r c -> p j (r c)"), None))
 
             def t_bias(c):
+                room()
                 bank = bc_bf(4 * c, 4)
                 biases[c] = cst.tile([P, CH], BF16, name="biasbc")
                 evq.append(("s", biases[c][:], bank[:].rearrange("p j c -> p (j c)"), bsm[:, c:c + 1]))
@@ -358,12 +366,6 @@ def tile_adaptivelstmcell_pb_kernel(
             t_z(1, 0, zbT, 0, "s")
             t_z(1, 0, zbT, 1, "v")
             flush_ev()
-            bankr = ps_tp.tile([P, 2, P], BF16, name="tpr", tag="tp")
-            for gi in range(2):
-                nc.tensor.transpose(bankr[:, gi, :], Rw[:, gi, :], ident_b[:])
-            nc.vector.tensor_copy(out=cT[:], in_=bankr[:].rearrange("p g c -> p (g c)"))
-            nc.vector.tensor_tensor(out=bsumT[:], in0=cT[:, 128:160], in1=cT[:, 160:192], op=ALU.add)
-            nc.vector.tensor_copy(out=cTf[:], in_=cT[:])
 
             pend = []
             done = [0]
@@ -400,17 +402,31 @@ def tile_adaptivelstmcell_pb_kernel(
                         t_z(e[1], 1, zwT if e[1] == 0 else zbT, e[2], EV_Z[e[2]])
                     exdone[0] += 1
 
+            def const_prep():
+                room()
+                bankr = ps_tp.tile([P, 2, P], BF16, name="tpr", tag="tp")
+                for gi in range(2):
+                    nc.tensor.transpose(bankr[:, gi, :], Rw[:, gi, :], ident_b[:])
+                nc.vector.tensor_copy(out=cT[:], in_=bankr[:].rearrange("p g c -> p (g c)"))
+                nc.vector.tensor_tensor(out=bsumT[:], in0=cT[:, 128:160], in1=cT[:, 160:192], op=ALU.add)
+                nc.vector.tensor_copy(out=cTf[:], in_=cT[:])
+                t_bias(0)
+
             def pe_slot(n):
                 k = n // NB
                 r = n % NB
                 ev = EV_A if n < NB * NCH - 4 else EV_B
                 if n == 0:
+                    const_prep()
                     t_words(1, raws[1][:], 0, "s")
                     t_words(1, raws[1][:], 1, "v")
                 elif n == 1:
                     t_words(1, raws[1][:], 2, "s")
                     t_words(1, raws[1][:], 3, "v")
                     raws[4] = load_w(4)
+                    nc.sync.dma_start(out=stage_b(1), in_=rows4(hx))
+                    nc.sync.dma_start(out=stage_z(0, 1), in_=zw2[:, :, 512:1024])
+                    nc.sync.dma_start(out=stage_z(1, 1), in_=zb2[:, :, 512:1024])
                 elif n == 2:
                     t_words(2, raws[2][:], 0, "s")
                     t_words(2, raws[2][:], 1, "v")
@@ -419,7 +435,7 @@ def tile_adaptivelstmcell_pb_kernel(
                         t_words(k + 1, raws[k + 1][:], 3, ev[3])
                         if k + 4 < 2 * NCH:
                             raws[k + 4] = load_w(k + 4)
-                    if 1 <= k <= 4:
+                    if 3 <= k <= 6:
                         extra_job()
                 else:
                     if k + 2 < 2 * NCH:
@@ -433,7 +449,7 @@ def tile_adaptivelstmcell_pb_kernel(
                         t_bias(k + 1)
 
                 if r == 3:
-                    if 1 <= k <= 4:
+                    if 3 <= k <= 6:
                         extra_job()
 
 
@@ -451,9 +467,9 @@ def tile_adaptivelstmcell_pb_kernel(
                     quant_key(k + 1, 0, wcs[k + 1], wss[k + 1])
                 elif r == 2 and k + 1 < 2 * NCH:
                     quant_key(k + 1, 1, wcs[k + 1], wss[k + 1])
-                if r == 1 and k == 2:
+                if r == 1 and k == 4:
                     quant_key("h", 0, xc[1], xs[1])
-                if r == 1 and k == 3:
+                if r == 1 and k == 5:
                     quant_key("h", 1, xc[1], xs[1])
 
             def g_norm(i):
@@ -527,7 +543,6 @@ def tile_adaptivelstmcell_pb_kernel(
                     stats_jobs("i", 0, True)
 
             t_wab(0)
-            t_bias(0)
             flush_ev()
             pe_al(0)
             s_al(0)
@@ -552,16 +567,16 @@ def tile_adaptivelstmcell_pb_kernel(
             soall = tailp.tile([P, 8, B], F32, name="soall")
             wcb = tailp.tile([P, H], BF16, name="wcb")
             bcb = tailp.tile([P, H], BF16, name="bcb")
-            QORD = (2, 0, 1, 3)
-            NJ = 32
+            SEQ = [(hb, q) for hb in range(8) for q in (2, 0, 1)]
+            NJ = len(SEQ)
             aTs = {}
             bTs = {}
             Xs = {}
             gs = {}
             cxTs = {}
 
-            def hq(j):
-                return (j // 4, QORD[j % 4])
+            def flat(t):
+                return t[:].rearrange("p b c -> p (b c)")
 
             def n_norm(hb):
                 for bt in range(NB):
@@ -569,53 +584,54 @@ def tile_adaptivelstmcell_pb_kernel(
                     nc.vector.tensor_scalar(out=ap, in0=ap, scalar1=st["h"][0][:, bt:bt + 1],
                                             scalar2=st["h"][1][:, bt:bt + 1], op0=ALU.subtract, op1=ALU.mult)
 
-            def t_a(j):
-                (hb, q) = hq(j)
-                aTs[j] = psA.tile([P, NB, P], F32, name="aT")
+            def t_to(key, src, pool, nm, store):
+                (hb, q) = key
+                store[key] = pool.tile([P, NB, P], F32, name=nm)
                 for bt in range(NB):
                     col = bt * NCOL + q * H + hb * P
-                    nc.tensor.transpose(aTs[j][:, bt, :], Ut[:, col:col + P], ident_f[:])
-
-            def t_b(j):
-                (hb, q) = hq(j)
-                bTs[j] = psB.tile([P, NB, P], F32, name="bT")
-                for bt in range(NB):
-                    col = bt * NCOL + q * H + hb * P
-                    nc.tensor.transpose(bTs[j][:, bt, :], Vt[:, col:col + P], ident_f[:])
+                    nc.tensor.transpose(store[key][:, bt, :], src[:, col:col + P], ident_f[:])
 
             def t_cx(hb):
                 cxTs[hb] = psC.tile([P, NB, P], BF16, name="cxT")
                 for bt in range(NB):
                     nc.tensor.transpose(cxTs[hb][:, bt, :], cxs[:, bt, hb * P:(hb + 1) * P], ident_b[:])
 
-            def s_x(j):
-                (hb, q) = hq(j)
-                m = q * 8 + hb
-                Xs[j] = xp.tile([P, B], F32, name="X")
-                nc.scalar.activation(out=Xs[j][:], in_=bTs[j][:].rearrange("p b c -> p (b c)"), func=ACT.Identity,
-                                     scale=cTf[:, 64 + m:65 + m], bias=bsumT[:, m:m + 1])
-
-            def v_m(j):
-                (hb, q) = hq(j)
+            def s_x(key):
+                (hb, q) = key
                 m = q * 8 + hb
                 if q == 3:
-                    gs[j] = soall[:, hb, :]
+                    Xs[key] = soall[:, hb, :]
+                else:
+                    xt = xp.tile([P, B], F32, name="X")
+                    Xs[key] = xt[:]
+                if key in XV:
+                    nc.vector.tensor_scalar(out=Xs[key], in0=flat(bTs[key]), scalar1=cTf[:, 64 + m:65 + m],
+                                            scalar2=bsumT[:, m:m + 1], op0=ALU.mult, op1=ALU.add)
+                else:
+                    nc.scalar.activation(out=Xs[key], in_=flat(bTs[key]), func=ACT.Identity,
+                                         scale=cTf[:, 64 + m:65 + m], bias=bsumT[:, m:m + 1])
+
+            def v_m(key):
+                (hb, q) = key
+                m = q * 8 + hb
+                if q == 3:
+                    gs[key] = soall[:, hb, :]
                 else:
                     gt = gp.tile([P, B], F32, name="g%d" % q)
-                    gs[j] = gt[:]
-                nc.vector.scalar_tensor_tensor(out=gs[j], in0=aTs[j][:].rearrange("p b c -> p (b c)"),
-                                               scalar=cTf[:, 32 + m:33 + m], in1=Xs[j][:], op0=ALU.mult, op1=ALU.add)
+                    gs[key] = gt[:]
+                nc.vector.scalar_tensor_tensor(out=gs[key], in0=flat(aTs[key]), scalar=cTf[:, 32 + m:33 + m],
+                                               in1=Xs[key], op0=ALU.mult, op1=ALU.add)
 
-            def s_act(j):
-                nc.scalar.activation(out=gs[j], in_=gs[j], func=(ACT.Tanh if hq(j)[1] == 1 else ACT.Sigmoid))
+            def s_act(key):
+                nc.scalar.activation(out=gs[key], in_=gs[key], func=(ACT.Tanh if key[1] == 1 else ACT.Sigmoid))
 
-            def v_pq(hb):
-                nc.vector.tensor_tensor(out=gs[4 * hb], in0=gs[4 * hb], in1=cxTs[hb][:].rearrange("p b c -> p (b c)"),
-                                        op=ALU.mult)
-                nc.vector.tensor_tensor(out=gs[4 * hb + 1], in0=gs[4 * hb + 1], in1=gs[4 * hb + 2], op=ALU.mult)
+            def v_p(hb):
+                nc.vector.tensor_tensor(out=gs[(hb, 2)], in0=gs[(hb, 2)], in1=flat(cxTs[hb]), op=ALU.mult)
 
-            def v_c2(hb):
-                nc.vector.tensor_tensor(out=cTall[:, hb, :], in0=gs[4 * hb], in1=gs[4 * hb + 1], op=ALU.add)
+            def g_qc(hb):
+                eng = nc.gpsimd if hb < GLAST else nc.vector
+                eng.tensor_tensor(out=gs[(hb, 0)], in0=gs[(hb, 0)], in1=gs[(hb, 1)], op=ALU.mult)
+                eng.tensor_tensor(out=cTall[:, hb, :], in0=gs[(hb, 2)], in1=gs[(hb, 0)], op=ALU.add)
 
             def bc_tail(col0, dst):
                 bank = psC.tile([P, 8, P], BF16, name="cxT")
@@ -625,34 +641,36 @@ def tile_adaptivelstmcell_pb_kernel(
 
             bc_tail(96, wcb[:])
             bc_tail(104, bcb[:])
-            t_a(0)
-            t_a(1)
+            t_to(SEQ[0], Ut, psA, "aT", aTs)
+            t_to(SEQ[1], Ut, psA, "aT", aTs)
             n_norm(0)
             for j in range(-2, NJ + 3):
                 if 0 <= j + 2 < NJ:
-                    if (j + 2) % 4 == 0:
-                        t_cx((j + 2) // 4)
+                    key = SEQ[j + 2]
                     if j + 2 >= 2:
-                        t_a(j + 2)
-                    t_b(j + 2)
+                        t_to(key, Ut, psA, "aT", aTs)
+                    t_to(key, Vt, psB, "bT", bTs)
+                    if (j + 2) % 3 == 2:
+                        t_to((key[0], 3), Vt, psB, "bT", bTs)
+                        t_cx(key[0])
                 if 0 <= j + 1 < NJ:
-                    s_x(j + 1)
+                    s_x(SEQ[j + 1])
                 if 0 <= j - 1 < NJ:
-                    s_act(j - 1)
+                    s_act(SEQ[j - 1])
+                    if (j - 1) % 3 == 2:
+                        g_qc(SEQ[j - 1][0])
                 if 0 <= j < NJ:
-                    v_m(j)
-                    if j % 4 == 0 and j // 4 + 1 < 8:
-                        n_norm(j // 4 + 1)
-                if j >= 5 and (j - 5) % 4 == 0:
-                    v_pq((j - 5) // 4)
-                if j >= 6 and (j - 6) % 4 == 0:
-                    v_c2((j - 6) // 4)
+                    if j % 3 == 2:
+                        s_x((SEQ[j][0], 3))
+                    v_m(SEQ[j])
+                    if j % 3 == 0 and SEQ[j][0] + 1 < 8:
+                        n_norm(SEQ[j][0] + 1)
+                    if j % 3 == 2:
+                        v_p(SEQ[j][0])
 
-            s1c = keep.tile([P, NB], F32, name="s1c")
-            s2c = keep.tile([P, NB], F32, name="s2c")
             mec = keep.tile([P, NB], F32, name="mec")
-            msc = keep.tile([P, NB], F32, name="msc")
-            vac = keep.tile([P, NB], F32, name="vac")
+            exc = keep.tile([P, NB], F32, name="exc")
+            nvc = keep.tile([P, NB], F32, name="nvc")
             rsc = keep.tile([P, NB], F32, name="rsc")
             cbs = {}
             sbs = {}
@@ -663,41 +681,37 @@ def tile_adaptivelstmcell_pb_kernel(
             def tcr(bt):
                 return Ut[:, bt * NCOL + H:bt * NCOL + 2 * H]
 
-            def e_back(bt, src, pool, nm, store):
-                store[bt] = []
-                for hf in range(2):
-                    t = pool.tile([P, NB, P], F32, name=nm)
-                    store[bt].append(t)
-                    for i in range(4):
-                        nc.tensor.transpose(t[:, i, :], src[:, 4 * hf + i, bt * P:(bt + 1) * P], ident_f[:])
+            def e_back1(bt, hf, src, pool, nm, store):
+                t = pool.tile([P, NB, P], F32, name=nm)
+                store[(bt, hf)] = t
+                for i in range(4):
+                    nc.tensor.transpose(t[:, i, :], src[:, 4 * hf + i, bt * P:(bt + 1) * P], ident_f[:])
 
-            def flat(t):
-                return t[:].rearrange("p b c -> p (b c)")
-
-            def e_sums(bt):
-                for hf in range(2):
-                    nc.scalar.activation(out=junk[:, 0:CH], in_=flat(cbs[bt][hf]), func=ACT.Copy,
+            def e_sums(bt, hf):
+                if True:
+                    nc.scalar.activation(out=junk[:, 0:CH], in_=flat(cbs[(bt, hf)]), func=ACT.Copy, scale=1.0 / H,
                                          accum_out=sumC[:, bt, hf:hf + 1])
-                    nc.scalar.activation(out=junk[:, CH:2 * CH], in_=flat(cbs[bt][hf]), func=ACT.Square,
-                                         accum_out=sqC[:, bt, hf:hf + 1])
+                    nc.scalar.activation(out=junk[:, CH:2 * CH], in_=flat(cbs[(bt, hf)]), func=ACT.Square,
+                                         scale=1.0 / 32.0, accum_out=sqC[:, bt, hf:hf + 1])
 
-            def e_stats(bt):
+            def e_st(bt, i):
                 c1 = slice(bt, bt + 1)
-                nc.vector.tensor_tensor(out=s1c[:, c1], in0=sumC[:, bt, 0:1], in1=sumC[:, bt, 1:2], op=ALU.add)
-                nc.vector.tensor_tensor(out=s2c[:, c1], in0=sqC[:, bt, 0:1], in1=sqC[:, bt, 1:2], op=ALU.add)
-                nc.vector.tensor_scalar(out=mec[:, c1], in0=s1c[:, c1], scalar1=1.0 / H, scalar2=None, op0=ALU.mult)
-                nc.vector.tensor_tensor(out=msc[:, c1], in0=mec[:, c1], in1=mec[:, c1], op=ALU.mult)
-                nc.vector.scalar_tensor_tensor(out=vac[:, c1], in0=s2c[:, c1], scalar=1.0 / H, in1=msc[:, c1],
-                                               op0=ALU.mult, op1=ALU.subtract)
-                nc.vector.tensor_scalar(out=vac[:, c1], in0=vac[:, c1], scalar1=0.0, scalar2=EPS,
-                                        op0=ALU.max, op1=ALU.add)
-                nc.gpsimd.tensor_tensor(out=rsc[:, c1], in0=vac[:, c1], in1=neghalf[:, c1], op=ALU.pow)
+                if i == 0:
+                    nc.vector.tensor_tensor(out=mec[:, c1], in0=sumC[:, bt, 0:1], in1=sumC[:, bt, 1:2], op=ALU.add)
+                    nc.vector.scalar_tensor_tensor(out=exc[:, c1], in0=sqC[:, bt, 0:1], scalar=EPS,
+                                                   in1=sqC[:, bt, 1:2], op0=ALU.add, op1=ALU.add)
+                if i == 1:
+                    nc.vector.scalar_tensor_tensor(out=nvc[:, c1], in0=mec[:, c1], scalar=mec[:, c1], in1=exc[:, c1],
+                                                   op0=ALU.mult, op1=ALU.subtract)
+                if i == 2:
+                    nc.vector.tensor_scalar(out=nvc[:, c1], in0=nvc[:, c1], scalar1=-1.0, scalar2=EPS,
+                                            op0=ALU.mult, op1=ALU.max)
+                    nc.gpsimd.tensor_tensor(out=rsc[:, c1], in0=nvc[:, c1], in1=neghalf[:, c1], op=ALU.pow)
 
-            def e_a(bt):
-                for hf in range(2):
-                    nc.vector.scalar_tensor_tensor(out=cyr(bt)[:, hf * CH:(hf + 1) * CH], in0=flat(cbs[bt][hf]),
-                                                   scalar=mec[:, bt:bt + 1], in1=wcb[:, hf * CH:(hf + 1) * CH],
-                                                   op0=ALU.subtract, op1=ALU.mult)
+            def e_a(bt, hf):
+                nc.vector.scalar_tensor_tensor(out=cyr(bt)[:, hf * CH:(hf + 1) * CH], in0=flat(cbs[(bt, hf)]),
+                                               scalar=mec[:, bt:bt + 1], in1=wcb[:, hf * CH:(hf + 1) * CH],
+                                               op0=ALU.subtract, op1=ALU.mult)
 
             def e_cy(bt):
                 nc.vector.scalar_tensor_tensor(out=cyr(bt), in0=cyr(bt), scalar=rsc[:, bt:bt + 1], in1=bcb[:],
@@ -705,21 +719,51 @@ def tile_adaptivelstmcell_pb_kernel(
                 nc.sync.dma_start(out=out_1[bt * P:(bt + 1) * P, :], in_=cyr(bt))
                 nc.scalar.activation(out=tcr(bt), in_=cyr(bt), func=ACT.Tanh)
 
-            def e_hy(bt):
-                for hf in range(2):
-                    nc.vector.tensor_tensor(out=tcr(bt)[:, hf * CH:(hf + 1) * CH], in0=tcr(bt)[:, hf * CH:(hf + 1) * CH],
-                                            in1=flat(sbs[bt][hf]), op=ALU.mult)
-                nc.sync.dma_start(out=out_0[bt * P:(bt + 1) * P, :], in_=tcr(bt))
+            def e_hy(bt, hf):
+                nc.vector.tensor_tensor(out=tcr(bt)[:, hf * CH:(hf + 1) * CH], in0=tcr(bt)[:, hf * CH:(hf + 1) * CH],
+                                        in1=flat(sbs[(bt, hf)]), op=ALU.mult)
+                if hf == 1:
+                    nc.sync.dma_start(out=out_0[bt * P:(bt + 1) * P, :], in_=tcr(bt))
 
-            for t in range(NB + 3):
+            def o_t(hb):
+                t_to((hb, 3), Ut, psC, "cxT", aTs)
+
+            def o_m(hb):
+                v_m((hb, 3))
+
+            o_t(0)
+            o_t(1)
+            for t in range(NB + 1):
                 if t < NB:
-                    e_back(t, cTall, psA, "aT", cbs)
-                    e_sums(t)
-                if 0 <= t - 1 < NB:
-                    e_stats(t - 1)
-                    e_back(t - 1, soall, psB, "bT", sbs)
-                    e_a(t - 1)
-                if 0 <= t - 3 < NB:
-                    e_hy(t - 3)
-                if 0 <= t - 1 < NB:
-                    e_cy(t - 1)
+                    e_back1(t, 0, cTall, psA, "aT", cbs)
+                    e_sums(t, 0)
+                    o_m(2 * t)
+                if t > 0:
+                    e_st(t - 1, 0)
+                    e_a(t - 1, 0)
+                    e_st(t - 1, 1)
+                if t < NB:
+                    e_back1(t, 1, cTall, psA, "aT", cbs)
+                    e_sums(t, 1)
+                    if 2 * t + 2 < 8:
+                        o_t(2 * t + 2)
+                    o_m(2 * t + 1)
+                    if 2 * t + 3 < 8:
+                        o_t(2 * t + 3)
+                    s_act((2 * t, 3))
+                    s_act((2 * t + 1, 3))
+                if t > 0:
+                    e_a(t - 1, 1)
+                    e_st(t - 1, 2)
+                if t > 1:
+                    e_cy(t - 2)
+            e_back1(0, 0, soall, psB, "bT", sbs)
+            e_back1(0, 1, soall, psB, "bT", sbs)
+            e_hy(0, 0)
+            e_cy(NB - 1)
+            e_hy(0, 1)
+            for bt in range(1, NB):
+                e_back1(bt, 0, soall, psB, "bT", sbs)
+                e_back1(bt, 1, soall, psB, "bT", sbs)
+                e_hy(bt, 0)
+                e_hy(bt, 1)

@@ -16,20 +16,25 @@ P = 128
 B = 512
 K = 1024
 H = 1024
-NB = B // P
+NBT = B // P
 NCOL = 4 * H
 CH = 512
 NCH = NCOL // CH
+NUNIT = 2 * NCH * NBT
+NHB = H // P
 EPS = 1e-5
-LAG = 3
-PIN = True
-EV_A = ("s", "v", "s", "s")
-EV_B = ("s", "s", "s", "s")
-EV_X = ("s", "v", "s", "v")
-EV_Z = ("s", "v")
-GLAST = 7
-WAB_V = ()
-XV = ()
+GATE_I = 0
+GATE_J = 1
+GATE_F = 2
+GATE_O = 3
+
+COL_B_IH = 0
+COL_LN_I_W = 32
+COL_LN_H_W = 64
+COL_LN_C_W = 96
+COL_LN_C_B = 104
+COL_LN_I_B = 128
+COL_LN_H_B = 160
 
 FLOPS = 2 * 2 * B * NCOL * K + 16 * 2 * B * H * 128
 
@@ -39,731 +44,557 @@ def tile_adaptivelstmcell_pb_kernel(
     ln_i_w, ln_i_b, ln_h_w, ln_h_b, ln_c_w, ln_c_b, out_0, out_1,
 ):
     nc = tc.nc
-    with ExitStack() as ctx:
-        if PIN:
-            ctx.enter_context(tc.manual_schedule())
-        keep = ctx.enter_context(tc.tile_pool(name="keep", bufs=1))
-        cst = ctx.enter_context(tc.tile_pool(name="cst", bufs=2))
+    with ExitStack() as whole:
+        whole.enter_context(tc.manual_schedule())
+        keep = whole.enter_context(tc.tile_pool(name="keep", bufs=1))
 
-        Ut = keep.tile([P, NB * NCOL], F32, name="Ut")
-        Vt = keep.tile([P, NB * NCOL], F32, name="Vt")
+        u_in = keep.tile([P, NBT * NCOL], F32, name="u_in")
+        u_hid = keep.tile([P, NBT * NCOL], F32, name="u_hid")
         ident_f = keep.tile([P, P], F32, name="ident_f")
         ident_b = keep.tile([P, P], BF16, name="ident_b")
-        xc = [keep.tile([P, 2, B], U32, name="xc%d" % h, align_bytes=64) for h in range(2)]
-        xs = [keep.tile([P, 2, B], U8, name="xs%d" % h, align_bytes=64) for h in range(2)]
-        zwT = keep.tile([P, 8, B], BF16, name="zwT")
-        zbT = keep.tile([P, 8, B], BF16, name="zbT")
-        Bz = keep.tile([P, CH], BF16, name="Bz")
-        Rw = keep.tile([P, 2, P], BF16, name="Rw")
-        cT = keep.tile([P, 2 * P], BF16, name="cT")
-        cTf = keep.tile([P, 2 * P], F32, name="cTf")
-        bsumT = keep.tile([P, 32], F32, name="bsumT")
-        neghalf = keep.tile([P, NB], F32, name="neghalf")
-        dmy = keep.tile([P, 1], F32, name="dmy")
-        sumU = keep.tile([P, 2, NB, NCH], F32, name="sumU")
-        sqU = keep.tile([P, 2, NB, NCH], F32, name="sqU")
-        bsm = keep.tile([P, NCH], F32, name="bsm")
-        btot = keep.tile([P, 1], F32, name="btot")
-        sumC = keep.tile([P, NB, 2], F32, name="sumC")
-        sqC = keep.tile([P, NB, 2], F32, name="sqC")
-        junk = keep.tile([P, H], BF16, name="junk")
+        act_words = [keep.tile([P, 2, B], U32, name="act_words%d" % h, align_bytes=64) for h in range(2)]
+        act_scales = [keep.tile([P, 2, B], U8, name="act_scales%d" % h, align_bytes=64) for h in range(2)]
+        zT = [keep.tile([P, 8, B], BF16, name="zT%d" % i) for i in range(2)]
+        b_hh_rows = keep.tile([P, CH], BF16, name="b_hh_rows")
+        vec_rows = keep.tile([P, 2, P], BF16, name="vec_rows")
+        vecT = keep.tile([P, 2 * P], BF16, name="vecT")
+        vecT_f = keep.tile([P, 2 * P], F32, name="vecT_f")
+        shiftT = keep.tile([P, 32], F32, name="shiftT")
+        neg_half = keep.tile([P, NBT], F32, name="neg_half")
+        warm = keep.tile([P, 1], F32, name="warm")
+        row_sum = keep.tile([P, 2, NBT, NCH], F32, name="row_sum")
+        row_sq = keep.tile([P, 2, NBT, NCH], F32, name="row_sq")
+        bias_sum = keep.tile([P, NCH], F32, name="bias_sum")
+        unused = keep.tile([P, H], BF16, name="unused")
 
-        vq = []
-        vqd = [0]
-        st = {}
-
-        def copy_on(eng, out, in_):
-            if eng == "s":
+        def copy_on(engine, out, in_):
+            if engine == "scalar":
                 nc.scalar.copy(out=out, in_=in_)
             else:
                 nc.vector.tensor_copy(out=out, in_=in_)
 
-        def stage_f(i):
-            return Vt[:, i * 2048:(i + 1) * 2048]
-
-        def stage_b(i):
-            return stage_f(i).bitcast(BF16).rearrange("p (r k) -> p r k", r=4)
-
-        def rows4(ap2d):
+        def rows_on_partitions(ap2d):
             return ap2d.rearrange("(r p) k -> p r k", p=P)
 
-        nc.vector.memset(neghalf[:], -0.5)
-        nc.scalar.activation(out=dmy[:], in_=neghalf[:, 0:1], func=ACT.Sigmoid)
-        nc.vector.memset(Rw[:], 0.0)
-        nc.vector.memset(Bz[:], 0.0)
+        def flat(t):
+            return t[:].rearrange("p b c -> p (b c)")
+
+        def layer_norm_scalars(name, total, total_sq, count, extra):
+            mean = keep.tile([P, NBT], F32, name="mean_" + name)
+            work = keep.tile([P, NBT], F32, name="work_" + name)
+            var = keep.tile([P, NBT], F32, name="var_" + name)
+            rstd = keep.tile([P, NBT], F32, name="rstd_" + name)
+            if extra is None:
+                nc.vector.tensor_scalar(out=mean[:], in0=total, scalar1=1.0 / count, scalar2=None, op0=ALU.mult)
+            else:
+                nc.vector.tensor_scalar(out=mean[:], in0=total, scalar1=extra, scalar2=1.0 / count,
+                                        op0=ALU.add, op1=ALU.mult)
+            nc.vector.tensor_tensor(out=work[:], in0=mean[:], in1=mean[:], op=ALU.mult)
+            nc.vector.scalar_tensor_tensor(out=var[:], in0=total_sq, scalar=1.0 / count, in1=work[:],
+                                           op0=ALU.mult, op1=ALU.subtract)
+            nc.vector.tensor_scalar(out=var[:], in0=var[:], scalar1=0.0, scalar2=EPS, op0=ALU.max, op1=ALU.add)
+            nc.gpsimd.tensor_tensor(out=rstd[:], in0=var[:], in1=neg_half[:], op=ALU.pow)
+            return (mean, rstd)
+
+        def half_scalars(half):
+            total = keep.tile([P, NBT], F32, name="total%d" % half)
+            total_sq = keep.tile([P, NBT], F32, name="total_sq%d" % half)
+            nc.vector.tensor_reduce(out=total[:], in_=row_sum[:, half, :, :], axis=AX.X, op=ALU.add)
+            nc.vector.tensor_reduce(out=total_sq[:], in_=row_sq[:, half, :, :], axis=AX.X, op=ALU.add)
+            extra = None
+            if half == 0:
+                bias_total = keep.tile([P, 1], F32, name="bias_total")
+                nc.vector.tensor_reduce(out=bias_total[:], in_=bias_sum[:], axis=AX.X, op=ALU.add)
+                extra = bias_total[:]
+            return layer_norm_scalars("half%d" % half, total[:], total_sq[:], NCOL, extra)
+
+        nc.vector.memset(neg_half[:], -0.5)
+        nc.scalar.activation(out=warm[:], in_=neg_half[:, 0:1], func=ACT.Sigmoid)
+        nc.vector.memset(vec_rows[:], 0.0)
+        nc.vector.memset(b_hh_rows[:], 0.0)
         make_identity(nc, ident_f[:])
         make_identity(nc, ident_b[:])
 
-        with ExitStack() as sctx:
-            ps_tp = sctx.enter_context(tc.psum_pool(name="ps_tp", bufs=2))
-            ps_xh = sctx.enter_context(tc.psum_pool(name="ps_xh", bufs=2))
-            ps_al = sctx.enter_context(tc.psum_pool(name="ps_al", bufs=2))
-            ps_be = sctx.enter_context(tc.psum_pool(name="ps_be", bufs=2))
-            rawp = sctx.enter_context(tc.tile_pool(name="rawp", bufs=3))
-            abp = sctx.enter_context(tc.tile_pool(name="abp", bufs=2))
-            grpp = sctx.enter_context(tc.tile_pool(name="grpp", bufs=3))
-            wqp = sctx.enter_context(tc.tile_pool(name="wqp", bufs=2))
-            wabp = sctx.enter_context(tc.tile_pool(name="wabp", bufs=2))
-            alp = sctx.enter_context(tc.tile_pool(name="alp", bufs=3))
+        with ExitStack() as stream:
+            ps_t = stream.enter_context(tc.psum_pool(name="ps_t", bufs=2))
+            ps_xh = stream.enter_context(tc.psum_pool(name="ps_xh", bufs=2))
+            ps_alpha = stream.enter_context(tc.psum_pool(name="ps_alpha", bufs=2))
+            ps_beta = stream.enter_context(tc.psum_pool(name="ps_beta", bufs=2))
+            raw_pool = stream.enter_context(tc.tile_pool(name="raw_pool", bufs=3))
+            hyper_raw_pool = stream.enter_context(tc.tile_pool(name="hyper_raw_pool", bufs=2))
+            grouped_pool = stream.enter_context(tc.tile_pool(name="grouped_pool", bufs=3))
+            mx_pool = stream.enter_context(tc.tile_pool(name="mx_pool", bufs=2))
+            hyper_pool = stream.enter_context(tc.tile_pool(name="hyper_pool", bufs=2))
+            alpha_pool = stream.enter_context(tc.tile_pool(name="alpha_pool", bufs=3))
+            bias_pool = stream.enter_context(tc.tile_pool(name="bias_pool", bufs=2))
 
-            def load_w(k):
-                w = w_ih if k < NCH else w_hh
-                c = k % NCH
-                raw = rawp.tile([P, 2048], F32, name="raww")
-                nc.sync.dma_start(
-                    out=raw[:].bitcast(BF16).rearrange("p (r k) -> p r k", r=4),
-                    in_=rows4(w[c * CH:(c + 1) * CH, :]),
-                )
-                return raw
+            def staged_words(i):
+                return u_hid[:, i * 2048:(i + 1) * 2048]
 
-            def load_ab(s):
-                ra = abp.tile([P, 8, P], BF16, name="rawa")
-                rb = abp.tile([P, 8, P], BF16, name="rawb")
-                nc.sync.dma_start(out=ra[:], in_=norm_alpha_w[s, :, :].rearrange("(r p) a -> p r a", p=P))
-                nc.sync.dma_start(out=rb[:], in_=bias_beta_w[s, :, :].rearrange("(r p) a -> p r a", p=P))
-                return (ra, rb)
+            def staged_z(i, part):
+                first = 4096 + (2 * i + part) * 1024
+                return u_hid[:, first:first + 1024].bitcast(BF16).rearrange("p (r k) -> p r k", r=NBT)
 
-            def mx_half(src, g, engs):
-                grp = grpp.tile([P, 2048], BF16, name="grp", align_bytes=64)
-                gview = grp[:].bitcast(F32).rearrange("p (n u) -> p n u", u=2)
-                for rp in range(2):
-                    bank = ps_tp.tile([P, 2, 2, P], F32, name="tpw", tag="tp")
-                    for u in range(2):
-                        for r2 in range(2):
-                            col = (2 * rp + r2) * 512 + 256 * g + 128 * u
-                            nc.tensor.transpose(bank[:, u, r2, :], src[:, col:col + P], ident_f[:])
-                    copy_on(engs[rp], gview[:, 256 * rp:256 * rp + 256, :],
-                            bank[:].rearrange("p u r c -> p (r c) u"))
-                return grp
+            z_rows = [rows_on_partitions(z.rearrange("b s a -> b (s a)")) for z in (zw, zb)]
 
-            def quant(grp, codes, scales, g):
-                nc.vector.quantize_mx(out=codes[:, g, :].bitcast(FP8X4), scales=scales[:, g, :], in_=grp[:])
+            def load_words(dst, src):
+                nc.sync.dma_start(out=dst.bitcast(BF16).rearrange("p (r k) -> p r k", r=4), in_=rows_on_partitions(src))
 
-            def prep_z(i, dstT, s0, bp, eng):
-                srcb = stage_b(i)
-                bank = ps_tp.tile([P, 4, 2, P], BF16, name="tpz", tag="tp")
-                for s in range(4):
-                    for bl in range(2):
-                        nc.tensor.transpose(bank[:, s, bl, :],
-                                            srcb[:, 2 * bp + bl, (s0 + s) * P:(s0 + s + 1) * P], ident_b[:])
-                copy_on(eng, dstT[:, s0:s0 + 4, 256 * bp:256 * bp + 256],
-                        bank[:].rearrange("p s l b -> p s (l b)"))
+            def load_z(i, part):
+                nc.sync.dma_start(out=staged_z(i, part), in_=z_rows[i][:, :, 512 * part:512 * (part + 1)])
 
-            def prep_wab(k, ab):
-                hh = k % 2
-                bank = ps_tp.tile([P, 2, 4, P], BF16, name="tpab", tag="tp")
-                for j in range(2):
-                    for r in range(4):
-                        nc.tensor.transpose(bank[:, j, r, :], ab[j][:, hh * 4 + r, :], ident_b[:])
-                wab = wabp.tile([P, 2, CH], BF16, name="wab")
-                nc.scalar.copy(out=wab[:], in_=bank[:].rearrange("p j r c -> p j (r c)"))
-                return wab
+            raw = {}
+            hyper_raw = {}
 
-            def bc_bf(col0, n):
-                bank = ps_tp.tile([P, n, P], BF16, name="tpc", tag="tp")
-                for j in range(n):
-                    nc.tensor.transpose(bank[:, j, :], cT[:, col0 + j:col0 + j + 1].to_broadcast([P, P]),
-                                        ident_b[:])
-                return bank
+            def load_weights(c):
+                if c < 2 * NCH:
+                    w = w_ih if c < NCH else w_hh
+                    raw[c] = raw_pool.tile([P, 2048], F32, name="raw")
+                    load_words(raw[c][:], w[(c % NCH) * CH:(c % NCH + 1) * CH, :])
 
-            def prep_bias(c):
-                bank = bc_bf(4 * c, 4)
-                t = cst.tile([P, CH], BF16, name="biasbc")
-                nc.scalar.activation(out=t[:], in_=bank[:].rearrange("p j c -> p (j c)"), func=ACT.Copy,
-                                     accum_out=bsm[:, c:c + 1])
-                return t
+            def load_hyper(s):
+                if s < 8:
+                    ra = hyper_raw_pool.tile([P, 8, P], BF16, name="raw_alpha")
+                    rb = hyper_raw_pool.tile([P, 8, P], BF16, name="raw_beta")
+                    nc.sync.dma_start(out=ra[:], in_=norm_alpha_w[s, :, :].rearrange("(r p) a -> p r a", p=P))
+                    nc.sync.dma_start(out=rb[:], in_=bias_beta_w[s, :, :].rearrange("(r p) a -> p r a", p=P))
+                    hyper_raw[s] = (ra, rb)
 
-            def prep_w(col0, c):
-                bank = bc_bf(col0 + 4 * c, 4)
-                t = cst.tile([P, CH], BF16, name="wbc", bufs=3)
-                nc.scalar.copy(out=t[:], in_=bank[:].rearrange("p j c -> p (j c)"))
-                return t
+            waiting = []
+            grouped = {}
+            w_words = {}
+            w_scales = {}
+            hyper = {}
+            bias_rows = {}
 
-            def prep_bsum(c):
-                bank = ps_tp.tile([P, 4, P], F32, name="tpf", tag="tp")
-                for j in range(4):
-                    nc.tensor.transpose(bank[:, j, :],
-                                        bsumT[:, 4 * c + j:4 * c + j + 1].to_broadcast([P, P]), ident_f[:])
-                t = cst.tile([P, CH], F32, name="bsb", bufs=3)
-                nc.scalar.copy(out=t[:], in_=bank[:].rearrange("p j c -> p (j c)"))
-                return t
-
-            def stats_tail(nm, s1, s2, inv_n, shift):
-                mean = keep.tile([P, NB], F32, name="mean_" + nm)
-                msq = keep.tile([P, NB], F32, name="msq_" + nm)
-                var = keep.tile([P, NB], F32, name="var_" + nm)
-                rstd = keep.tile([P, NB], F32, name="rstd_" + nm)
-                st[nm] = (mean, rstd)
-
-                def j_mean():
-                    if shift is None:
-                        nc.vector.tensor_scalar(out=mean[:], in0=s1, scalar1=inv_n, scalar2=None, op0=ALU.mult)
+            def copy_waiting():
+                for (engine, out, in_, accum_out) in waiting:
+                    if accum_out is None:
+                        copy_on(engine, out, in_)
                     else:
-                        nc.vector.tensor_scalar(out=mean[:], in0=s1, scalar1=shift, scalar2=inv_n,
-                                                op0=ALU.add, op1=ALU.mult)
+                        nc.scalar.activation(out=out, in_=in_, func=ACT.Copy, accum_out=accum_out)
+                waiting[:] = []
 
-                def j_msq():
-                    nc.vector.tensor_tensor(out=msq[:], in0=mean[:], in1=mean[:], op=ALU.mult)
+            def new_bank(shape, dtype):
+                if len(waiting) == 2:
+                    copy_waiting()
+                return ps_t.tile(shape, dtype, name="bank")
 
-                def j_var():
-                    nc.vector.scalar_tensor_tensor(out=var[:], in0=s2, scalar=inv_n, in1=msq[:],
-                                                   op0=ALU.mult, op1=ALU.subtract)
-
-                def j_rstd():
-                    nc.vector.tensor_scalar(out=var[:], in0=var[:], scalar1=0.0, scalar2=EPS,
-                                            op0=ALU.max, op1=ALU.add)
-                    nc.gpsimd.tensor_tensor(out=rstd[:], in0=var[:], in1=neghalf[:], op=ALU.pow)
-
-                vq.extend([j_mean, j_msq, j_var, j_rstd])
-
-            def stats_jobs(nm, half, with_shift):
-                s1 = keep.tile([P, NB], F32, name="s1_" + nm)
-                s2 = keep.tile([P, NB], F32, name="s2_" + nm)
-
-                def j_s1():
-                    nc.vector.tensor_reduce(out=s1[:], in_=sumU[:, half, :, :], axis=AX.X, op=ALU.add)
-
-                def j_s2():
-                    nc.vector.tensor_reduce(out=s2[:], in_=sqU[:, half, :, :], axis=AX.X, op=ALU.add)
-
-                def j_bt():
-                    nc.vector.tensor_reduce(out=btot[:], in_=bsm[:], axis=AX.X, op=ALU.add)
-
-                vq.extend([j_s1, j_s2])
-                if with_shift:
-                    vq.append(j_bt)
-                stats_tail(nm, s1[:], s2[:], 1.0 / NCOL, btot[:, 0:1] if with_shift else None)
-
-            def seg_of(T, bt, c):
-                return T[:, bt * NCOL + c * CH:bt * NCOL + (c + 1) * CH]
-
-            zw2 = rows4(zw.rearrange("b s a -> b (s a)"))
-            zb2 = rows4(zb.rearrange("b s a -> b (s a)"))
-
-            def stage_z(i, hf):
-                return Vt[:, 4096 + (2 * i + hf) * 1024:4096 + (2 * i + hf + 1) * 1024].bitcast(BF16).rearrange(
-                    "p (r k) -> p r k", r=4)
-
-            raws = {}
-            abs_ = {}
-            nc.sync.dma_start(out=stage_b(0), in_=rows4(x))
-            raws[0] = load_w(0)
-            nc.sync.dma_start(out=stage_z(0, 0), in_=zw2[:, :, 0:512])
-            nc.sync.dma_start(out=stage_z(1, 0), in_=zb2[:, :, 0:512])
-            abs_[0] = load_ab(0)
-            raws[1] = load_w(1)
-            for (gi, r0, vec) in ((0, 0, b_ih), (0, 32, ln_i_w), (0, 64, ln_h_w), (0, 96, ln_c_w),
-                                  (0, 104, ln_c_b), (1, 0, ln_i_b), (1, 32, ln_h_b)):
-                m = vec.shape[0] // P
-                nc.sync.dma_start(out=Rw[r0:r0 + m, gi, :], in_=vec.rearrange("(m p) -> m p", p=P))
-            nc.sync.dma_start(out=Bz[0:NCH, :], in_=b_hh.rearrange("(c n) -> c n", c=NCH))
-            abs_[1] = load_ab(1)
-            raws[2] = load_w(2)
-
-            wcs = {}
-            wss = {}
-            wabs = {}
-            biases = {}
-            ficst = {}
-            grps = {}
-            evq = []
-            evdone = [0]
-
-            def flush_ev():
-                while evdone[0] < len(evq):
-                    (eng, out, in_, acc) = evq[evdone[0]]
-                    if acc is not None:
-                        nc.scalar.activation(out=out, in_=in_, func=ACT.Copy, accum_out=acc)
-                    else:
-                        copy_on(eng, out, in_)
-                    evdone[0] += 1
-
-            def room():
-                if len(evq) - evdone[0] >= 2:
-                    flush_ev()
-
-            def new_wq(k):
-                wcs[k] = wqp.tile([P, 2, CH], U32, name="wc", align_bytes=64)
-                wss[k] = wqp.tile([P, 2, CH], U8, name="ws", align_bytes=64)
-
-            def t_words(key, src, j, eng):
+            def transpose_words(operand, src, j, engine):
                 g = j // 2
-                rp = j % 2
-                if rp == 0:
-                    grps[(key, g)] = grpp.tile([P, 2048], BF16, name="grp", align_bytes=64)
-                gview = grps[(key, g)][:].bitcast(F32).rearrange("p (n u) -> p n u", u=2)
-                room()
-                bank = ps_tp.tile([P, 2, 2, P], F32, name="tpw", tag="tp")
+                h = j % 2
+                if h == 0:
+                    grouped[(operand, g)] = grouped_pool.tile([P, 4 * CH], BF16, name="grouped", align_bytes=64)
+                bank = new_bank([P, 2, 2, P], F32)
                 for u in range(2):
-                    for r2 in range(2):
-                        col = (2 * rp + r2) * 512 + 256 * g + 128 * u
-                        nc.tensor.transpose(bank[:, u, r2, :], src[:, col:col + P], ident_f[:])
-                evq.append((eng, gview[:, 256 * rp:256 * rp + 256, :],
-                            bank[:].rearrange("p u r c -> p (r c) u"), None))
+                    for r in range(2):
+                        first = (2 * h + r) * 512 + 256 * g + 128 * u
+                        nc.tensor.transpose(bank[:, u, r, :], src[:, first:first + P], ident_f[:])
+                pairs = grouped[(operand, g)][:].bitcast(F32).rearrange("p (n u) -> p n u", u=2)
+                waiting.append((engine, pairs[:, 256 * h:256 * (h + 1), :], bank[:].rearrange("p u r c -> p (r c) u"), None))
 
-            def t_z(i, hf, dstT, bp, eng):
-                srcb = stage_z(i, hf)
-                room()
-                bank = ps_tp.tile([P, 4, 2, P], BF16, name="tpz", tag="tp")
+            def quantise(operand, g, words, scales):
+                nc.vector.quantize_mx(out=words[:, g, :].bitcast(FP8X4), scales=scales[:, g, :],
+                                      in_=grouped[(operand, g)][:])
+
+            def transpose_z(i, part, pair, engine):
+                src = staged_z(i, part)
+                bank = new_bank([P, 4, 2, P], BF16)
                 for s in range(4):
-                    for bl in range(2):
-                        nc.tensor.transpose(bank[:, s, bl, :], srcb[:, 2 * bp + bl, s * P:(s + 1) * P], ident_b[:])
-                evq.append((eng, dstT[:, 4 * hf:4 * hf + 4, 256 * bp:256 * bp + 256],
-                            bank[:].rearrange("p s l b -> p s (l b)"), None))
+                    for t in range(2):
+                        nc.tensor.transpose(bank[:, s, t, :], src[:, 2 * pair + t, s * P:(s + 1) * P], ident_b[:])
+                waiting.append((engine, zT[i][:, 4 * part:4 * part + 4, 256 * pair:256 * (pair + 1)],
+                                bank[:].rearrange("p s t b -> p s (t b)"), None))
 
-            def t_wab(k):
-                ab = abs_[k // 2]
-                hh = k % 2
-                room()
-                bank = ps_tp.tile([P, 2, 4, P], BF16, name="tpab", tag="tp")
-                for j in range(2):
+            def transpose_hyper(c):
+                bank = new_bank([P, 2, 4, P], BF16)
+                for i in range(2):
                     for r in range(4):
-                        nc.tensor.transpose(bank[:, j, r, :], ab[j][:, hh * 4 + r, :], ident_b[:])
-                wabs[k] = wabp.tile([P, 2, CH], BF16, name="wab")
-                evq.append(("v" if k in WAB_V else "s", wabs[k][:], bank[:].rearrange("p j r c -> p j (r c)"), None))
+                        nc.tensor.transpose(bank[:, i, r, :], hyper_raw[c // 2][i][:, (c % 2) * 4 + r, :], ident_b[:])
+                hyper[c] = hyper_pool.tile([P, 2, CH], BF16, name="hyper")
+                waiting.append(("scalar", hyper[c][:], bank[:].rearrange("p i r c -> p i (r c)"), None))
 
-            def t_bias(c):
-                room()
-                bank = bc_bf(4 * c, 4)
-                biases[c] = cst.tile([P, CH], BF16, name="biasbc")
-                evq.append(("s", biases[c][:], bank[:].rearrange("p j c -> p (j c)"), bsm[:, c:c + 1]))
+            def transpose_vectors():
+                bank = new_bank([P, 2, P], BF16)
+                for i in range(2):
+                    nc.tensor.transpose(bank[:, i, :], vec_rows[:, i, :], ident_b[:])
+                nc.vector.tensor_copy(out=vecT[:], in_=bank[:].rearrange("p i c -> p (i c)"))
+                nc.vector.tensor_tensor(out=shiftT[:], in0=vecT[:, COL_LN_I_B:COL_LN_I_B + 32],
+                                        in1=vecT[:, COL_LN_H_B:COL_LN_H_B + 32], op=ALU.add)
+                nc.vector.tensor_copy(out=vecT_f[:], in_=vecT[:])
 
-            def t_w(col0, c, store):
-                bank = bc_bf(col0 + 4 * c, 4)
-                store[c] = cst.tile([P, CH], BF16, name="wbc", bufs=3)
-                evq.append(("s", store[c][:], bank[:].rearrange("p j c -> p (j c)"), None))
+            def spread_bias(c):
+                bank = new_bank([P, 4, P], BF16)
+                for m in range(4):
+                    col = COL_B_IH + 4 * c + m
+                    nc.tensor.transpose(bank[:, m, :], vecT[:, col:col + 1].to_broadcast([P, P]), ident_b[:])
+                bias_rows[c] = bias_pool.tile([P, CH], BF16, name="bias_rows")
+                waiting.append(("scalar", bias_rows[c][:], bank[:].rearrange("p m c -> p (m c)"), bias_sum[:, c:c + 1]))
 
-            def t_bsum(c, store):
-                bank = ps_tp.tile([P, 4, P], F32, name="tpf", tag="tp")
-                for j in range(4):
-                    nc.tensor.transpose(bank[:, j, :],
-                                        bsumT[:, 4 * c + j:4 * c + j + 1].to_broadcast([P, P]), ident_f[:])
-                store[c] = cst.tile([P, CH], F32, name="bsb", bufs=3)
-                evq.append(("s", store[c][:], bank[:].rearrange("p j c -> p (j c)"), None))
+            load_words(staged_words(0), x)
+            load_weights(0)
+            load_z(0, 0)
+            load_z(1, 0)
+            load_hyper(0)
+            load_weights(1)
+            for (i, row, vec) in ((0, COL_B_IH, b_ih), (0, COL_LN_I_W, ln_i_w), (0, COL_LN_H_W, ln_h_w),
+                                  (0, COL_LN_C_W, ln_c_w), (0, COL_LN_C_B, ln_c_b),
+                                  (1, COL_LN_I_B - P, ln_i_b), (1, COL_LN_H_B - P, ln_h_b)):
+                nc.sync.dma_start(out=vec_rows[row:row + vec.shape[0] // P, i, :], in_=vec.rearrange("(m p) -> m p", p=P))
+            nc.sync.dma_start(out=b_hh_rows[0:NCH, :], in_=b_hh.rearrange("(c n) -> c n", c=NCH))
+            load_hyper(1)
+            load_weights(2)
 
-            def quant_key(key, g, codes, scales):
-                quant(grps[(key, g)], codes, scales, g)
+            def new_mx_tiles(c):
+                w_words[c] = mx_pool.tile([P, 2, CH], U32, name="w_words", align_bytes=64)
+                w_scales[c] = mx_pool.tile([P, 2, CH], U8, name="w_scales", align_bytes=64)
 
             for j in range(4):
-                t_words("x", stage_f(0), j, "sv"[j % 2])
-                if j % 2 == 1:
-                    flush_ev()
-            quant_key("x", 0, xc[0], xs[0])
-            new_wq(0)
-            t_words(0, raws[0][:], 0, "s")
-            t_words(0, raws[0][:], 1, "v")
-            flush_ev()
-            quant_key("x", 1, xc[0], xs[0])
-            t_words(0, raws[0][:], 2, "s")
-            t_words(0, raws[0][:], 3, "v")
-            flush_ev()
-            quant_key(0, 0, wcs[0], wss[0])
-            raws[3] = load_w(3)
-            t_z(0, 0, zwT, 0, "s")
-            t_z(0, 0, zwT, 1, "v")
-            flush_ev()
-            quant_key(0, 1, wcs[0], wss[0])
-            t_z(1, 0, zbT, 0, "s")
-            t_z(1, 0, zbT, 1, "v")
-            flush_ev()
+                transpose_words("x", staged_words(0), j, ("scalar", "vector")[j % 2])
+            copy_waiting()
+            quantise("x", 0, act_words[0], act_scales[0])
+            new_mx_tiles(0)
+            for j in range(4):
+                transpose_words(0, raw[0][:], j, ("scalar", "vector")[j % 2])
+                if j == 1:
+                    copy_waiting()
+                    quantise("x", 1, act_words[0], act_scales[0])
+            copy_waiting()
+            quantise(0, 0, w_words[0], w_scales[0])
+            load_weights(3)
+            for i in range(2):
+                transpose_z(i, 0, 0, "scalar")
+                transpose_z(i, 0, 1, "vector")
+                copy_waiting()
+                if i == 0:
+                    quantise(0, 1, w_words[0], w_scales[0])
+            transpose_hyper(0)
+            copy_waiting()
 
-            pend = []
-            done = [0]
-            als = {}
-            alsb = {}
-            fiw = {}
-            fib = {}
-            NU = 2 * NCH * NB
-            extras = [("x", 0), ("x", 1), ("x", 2), ("x", 3), ("z", 0, 0), ("z", 0, 1), ("z", 1, 0), ("z", 1, 1)]
-            exdone = [0]
+            alpha_ps = {}
+            alpha_sb = {}
+            beta_ps = {}
 
-            def emit_sq(upto):
-                while done[0] < min(upto, len(pend)):
-                    (seg, acc) = pend[done[0]]
-                    nc.scalar.activation(out=junk[:, 0:CH], in_=seg, func=ACT.Square, accum_out=acc)
-                    done[0] += 1
+            def where(n):
+                c = n // NBT
+                bt = n % NBT
+                half = c // NCH
+                first = bt * NCOL + (c % NCH) * CH
+                return (c, bt, half, (u_in, u_hid)[half][:, first:first + CH])
 
-            def pe_al(n):
-                k = n // NB
-                b0 = (n % NB) * P
-                als[n] = ps_al.tile([P, CH], F32, name="al")
-                nc.tensor.matmul(als[n][:], lhsT=zwT[:, k // 2, b0:b0 + P], rhs=wabs[k][:, 0, :], start=True, stop=True)
+            def alpha_of(n):
+                (c, bt, half, u) = where(n)
+                alpha_ps[n] = ps_alpha.tile([P, CH], F32, name="alpha_ps")
+                nc.tensor.matmul(alpha_ps[n][:], lhsT=zT[0][:, c // 2, bt * P:(bt + 1) * P], rhs=hyper[c][:, 0, :],
+                                 start=True, stop=True)
+                alpha_sb[n] = alpha_pool.tile([P, CH], F32, name="alpha_sb")
+                nc.scalar.copy(out=alpha_sb[n][:], in_=alpha_ps[n][:])
 
-            def s_al(n):
-                alsb[n] = alp.tile([P, CH], F32, name="al_sb")
-                nc.scalar.copy(out=alsb[n][:], in_=als[n][:])
-
-            def extra_job():
-                if exdone[0] < len(extras):
-                    e = extras[exdone[0]]
-                    if e[0] == "x":
-                        t_words("h", stage_f(1), e[1], EV_X[e[1]])
-                    else:
-                        t_z(e[1], 1, zwT if e[1] == 0 else zbT, e[2], EV_Z[e[2]])
-                    exdone[0] += 1
-
-            def const_prep():
-                room()
-                bankr = ps_tp.tile([P, 2, P], BF16, name="tpr", tag="tp")
-                for gi in range(2):
-                    nc.tensor.transpose(bankr[:, gi, :], Rw[:, gi, :], ident_b[:])
-                nc.vector.tensor_copy(out=cT[:], in_=bankr[:].rearrange("p g c -> p (g c)"))
-                nc.vector.tensor_tensor(out=bsumT[:], in0=cT[:, 128:160], in1=cT[:, 160:192], op=ALU.add)
-                nc.vector.tensor_copy(out=cTf[:], in_=cT[:])
-                t_bias(0)
-
-            def pe_slot(n):
-                k = n // NB
-                r = n % NB
-                ev = EV_A if n < NB * NCH - 4 else EV_B
+            def banks_of_step(n):
+                c = n // NBT
+                r = n % NBT
+                second = "vector" if c < NCH - 1 else "scalar"
                 if n == 0:
-                    const_prep()
-                    t_words(1, raws[1][:], 0, "s")
-                    t_words(1, raws[1][:], 1, "v")
-                elif n == 1:
-                    t_words(1, raws[1][:], 2, "s")
-                    t_words(1, raws[1][:], 3, "v")
-                    raws[4] = load_w(4)
-                    nc.sync.dma_start(out=stage_b(1), in_=rows4(hx))
-                    nc.sync.dma_start(out=stage_z(0, 1), in_=zw2[:, :, 512:1024])
-                    nc.sync.dma_start(out=stage_z(1, 1), in_=zb2[:, :, 512:1024])
-                elif n == 2:
-                    t_words(2, raws[2][:], 0, "s")
-                    t_words(2, raws[2][:], 1, "v")
-                elif r == 0:
-                    if k + 1 < 2 * NCH:
-                        t_words(k + 1, raws[k + 1][:], 3, ev[3])
-                        if k + 4 < 2 * NCH:
-                            raws[k + 4] = load_w(k + 4)
-                    if 3 <= k <= 6:
-                        extra_job()
-                else:
-                    if k + 2 < 2 * NCH:
-                        t_words(k + 2, raws[k + 2][:], r - 1, ev[r - 1])
-                if r == 1 and k + 1 < 2 * NCH:
-                    t_wab(k + 1)
-                    if (k + 1) % 2 == 1 and (k + 1) // 2 + 2 < 8:
-                        abs_[(k + 1) // 2 + 2] = load_ab((k + 1) // 2 + 2)
-                if r == 2:
-                    if k + 1 < NCH:
-                        t_bias(k + 1)
+                    transpose_vectors()
+                    spread_bias(0)
+                    for j in range(4):
+                        transpose_words(1, raw[1][:], j, ("scalar", "vector")[j % 2])
+                    load_weights(4)
+                    load_words(staged_words(1), hx)
+                    load_z(0, 1)
+                    load_z(1, 1)
+                elif r == 0 and c + 1 < 2 * NCH:
+                    transpose_words(c + 1, raw[c + 1][:], 3, second)
+                    load_weights(c + 4)
+                elif r > 0 and c + 2 < 2 * NCH:
+                    transpose_words(c + 2, raw[c + 2][:], r - 1, ("scalar", second, "scalar")[r - 1])
+                if r == 1 and c + 1 < 2 * NCH:
+                    transpose_hyper(c + 1)
+                    if c % 2 == 0:
+                        load_hyper(c // 2 + 2)
+                if r == 2 and c + 1 < NCH:
+                    spread_bias(c + 1)
+                if 3 <= c <= 6 and r in (0, 3):
+                    e = 2 * (c - 3) + r // 3
+                    if e < 4:
+                        transpose_words("hx", staged_words(1), e, ("scalar", "vector")[e % 2])
+                    else:
+                        transpose_z((e - 4) // 2, 1, e % 2, ("scalar", "vector")[e % 2])
 
-                if r == 3:
-                    if 3 <= k <= 6:
-                        extra_job()
-
-
-            def v_quants(n):
-                k = n // NB
-                r = n % NB
-                if k == 0:
+            def quantise_in_step(n):
+                c = n // NBT
+                r = n % NBT
+                if c + 1 < 2 * NCH and n > 0:
+                    if r == (1 if c == 0 else 0):
+                        new_mx_tiles(c + 1)
+                        quantise(c + 1, 0, w_words[c + 1], w_scales[c + 1])
                     if r == 2:
-                        new_wq(1)
-                        quant_key(1, 0, wcs[1], wss[1])
-                    if r == 3:
-                        quant_key(1, 1, wcs[1], wss[1])
-                elif r == 0 and k + 1 < 2 * NCH:
-                    new_wq(k + 1)
-                    quant_key(k + 1, 0, wcs[k + 1], wss[k + 1])
-                elif r == 2 and k + 1 < 2 * NCH:
-                    quant_key(k + 1, 1, wcs[k + 1], wss[k + 1])
-                if r == 1 and k == 4:
-                    quant_key("h", 0, xc[1], xs[1])
-                if r == 1 and k == 5:
-                    quant_key("h", 1, xc[1], xs[1])
+                        quantise(c + 1, 1, w_words[c + 1], w_scales[c + 1])
+                if r == 1 and c in (4, 5):
+                    quantise("hx", c - 4, act_words[1], act_scales[1])
 
-            def g_norm(i):
-                bt = i % NB
-                o = bt * NCOL + (i // NB) * H
-                nc.vector.tensor_scalar(out=Ut[:, o:o + H], in0=Ut[:, o:o + H], scalar1=st["i"][0][:, bt:bt + 1],
-                                        scalar2=st["i"][1][:, bt:bt + 1], op0=ALU.subtract, op1=ALU.mult)
-
-            def drip(m):
-                for t in range(m):
-                    if vqd[0] < len(vq):
-                        vq[vqd[0]]()
-                        vqd[0] += 1
-
-            bes = {}
-            segs = {}
-            fid = [0]
-            FI0 = NB * NCH + 3
-
-            def v_c(n):
-                k = n // NB
-                half = k // NCH
-                nc.vector.scalar_tensor_tensor(out=segs[n], in0=segs[n], scalar=1.0, in1=bes[n][:], op0=ALU.mult,
-                                               op1=ALU.add, accum_out=sumU[:, half, n % NB, k % NCH:k % NCH + 1])
+            def add_beta(n):
+                (c, bt, half, u) = where(n)
+                nc.vector.scalar_tensor_tensor(out=u, in0=u, scalar=1.0, in1=beta_ps[n][:], op0=ALU.mult, op1=ALU.add,
+                                               accum_out=row_sum[:, half, bt, c % NCH:c % NCH + 1])
                 if half == 0:
-                    nc.gpsimd.tensor_tensor(out=segs[n], in0=segs[n], in1=biases[k][:], op=ALU.add)
-                pend.append((segs[n], sqU[:, half, n % NB, k % NCH:k % NCH + 1]))
+                    nc.gpsimd.tensor_tensor(out=u, in0=u, in1=bias_rows[c][:], op=ALU.add)
 
-            def step(n):
-                k = n // NB
-                bt = n % NB
-                half = k // NCH
-                c = k % NCH
-                segs[n] = seg_of(Ut if half == 0 else Vt, bt, c)
-                b0 = bt * P
+            def sum_squares(n):
+                (c, bt, half, u) = where(n)
+                nc.scalar.activation(out=unused[:, 0:CH], in_=u, func=ACT.Square,
+                                     accum_out=row_sq[:, half, bt, c % NCH:c % NCH + 1])
+
+            def normalise_input_half(i):
+                bt = i % NBT
+                first = bt * NCOL + (i // NBT) * H
+                nc.vector.tensor_scalar(out=u_in[:, first:first + H], in0=u_in[:, first:first + H],
+                                        scalar1=scal_in[0][:, bt:bt + 1], scalar2=scal_in[1][:, bt:bt + 1],
+                                        op0=ALU.subtract, op1=ALU.mult)
+
+            FIRST_HID = NCH * NBT
+            scal_in = None
+            alpha_of(0)
+            for n in range(NUNIT):
+                (c, bt, half, u) = where(n)
+                rows = slice(bt * P, (bt + 1) * P)
                 xh = ps_xh.tile([P, CH], F32, name="xh")
                 for g in range(2):
                     nc.tensor.matmul_mx(
                         out=xh[:],
-                        lhsT=xc[half][:, g, b0:b0 + P].bitcast(FP8X4),
-                        lhsT_scale=xs[half][:, g, b0:b0 + P],
-                        rhs=wcs[k][:, g, :].bitcast(FP8X4),
-                        rhs_scale=wss[k][:, g, :],
+                        lhsT=act_words[half][:, g, rows].bitcast(FP8X4),
+                        lhsT_scale=act_scales[half][:, g, rows],
+                        rhs=w_words[c][:, g, :].bitcast(FP8X4),
+                        rhs_scale=w_scales[c][:, g, :],
                         start=(g == 0),
                         stop=(g == 1),
                     )
-                flush_ev()
-                if n + 1 < NU:
-                    pe_al(n + 1)
-                    s_al(n + 1)
-                pe_slot(n)
-                bes[n] = ps_be.tile([P, CH], F32, name="be")
-                nc.tensor.matmul(bes[n][:], lhsT=zbT[:, k // 2, b0:b0 + P], rhs=wabs[k][:, 1, :], start=True,
+                copy_waiting()
+                if n + 1 < NUNIT:
+                    alpha_of(n + 1)
+                banks_of_step(n)
+                beta_ps[n] = ps_beta.tile([P, CH], F32, name="beta_ps")
+                nc.tensor.matmul(beta_ps[n][:], lhsT=zT[1][:, c // 2, rows], rhs=hyper[c][:, 1, :], start=True,
                                  stop=(half == 0))
                 if half == 1:
-                    nc.tensor.matmul(bes[n][:], lhsT=ident_b[:, c:c + 1].to_broadcast([P, P]), rhs=Bz[:],
-                                     start=False, stop=True)
-                emit_sq(n - LAG + 1)
-                v_quants(n)
-                nc.vector.tensor_tensor(out=segs[n], in0=xh[:], in1=alsb[n][:], op=ALU.mult)
-                if n >= FI0 + 4 and fid[0] < 4 * NB:
-                    g_norm(fid[0])
-                    fid[0] += 1
-                else:
-                    drip(1)
-                if n > 0:
-                    v_c(n - 1)
-                drip(1)
-                if n == FI0 - 1:
-                    emit_sq(NB * NCH)
-                    stats_jobs("i", 0, True)
+                    nc.tensor.matmul(beta_ps[n][:], lhsT=ident_b[:, c % NCH:c % NCH + 1].to_broadcast([P, P]),
+                                     rhs=b_hh_rows[:], start=False, stop=True)
+                if n >= 3:
+                    sum_squares(n - 3)
+                quantise_in_step(n)
+                nc.vector.tensor_tensor(out=u, in0=xh[:], in1=alpha_sb[n][:], op=ALU.mult)
+                if FIRST_HID + 3 <= n < FIRST_HID + 3 + 4 * NBT:
+                    normalise_input_half(n - FIRST_HID - 3)
+                if n >= 1:
+                    add_beta(n - 1)
+                if n == FIRST_HID + 2:
+                    scal_in = half_scalars(0)
+            add_beta(NUNIT - 1)
+            for n in range(NUNIT - 3, NUNIT):
+                sum_squares(n)
+            scal_hid = half_scalars(1)
 
-            t_wab(0)
-            flush_ev()
-            pe_al(0)
-            s_al(0)
-            for n in range(NU):
-                step(n)
-            v_c(NU - 1)
+        with ExitStack() as tail:
+            tail_keep = tail.enter_context(tc.tile_pool(name="tail_keep", bufs=1))
+            part_pool = tail.enter_context(tc.tile_pool(name="part_pool", bufs=3))
+            gate_pool = tail.enter_context(tc.tile_pool(name="gate_pool", bufs=2))
+            ps_a = tail.enter_context(tc.psum_pool(name="ps_a", bufs=3))
+            ps_b = tail.enter_context(tc.psum_pool(name="ps_b", bufs=3))
+            ps_c = tail.enter_context(tc.psum_pool(name="ps_c", bufs=2))
+            cx_rows = tail_keep.tile([P, NBT, H], BF16, name="cx_rows")
+            nc.sync.dma_start(out=cx_rows[:], in_=rows_on_partitions(cx))
+            cellT = tail_keep.tile([P, NHB, B], F32, name="cellT")
+            outT = tail_keep.tile([P, NHB, B], F32, name="outT")
+            ln_c_w_rows = tail_keep.tile([P, H], BF16, name="ln_c_w_rows")
+            ln_c_b_rows = tail_keep.tile([P, H], BF16, name="ln_c_b_rows")
 
-            emit_sq(len(pend))
-            stats_jobs("h", 1, False)
-            drip(16)
+            in_T = {}
+            hid_T = {}
+            hid_part = {}
+            gate = {}
+            cxT = {}
 
-        with ExitStack() as tctx:
-            tailp = tctx.enter_context(tc.tile_pool(name="tailp", bufs=1))
-            xp = tctx.enter_context(tc.tile_pool(name="xp", bufs=3))
-            gp = tctx.enter_context(tc.tile_pool(name="gp", bufs=2))
-            psA = tctx.enter_context(tc.psum_pool(name="psA", bufs=3))
-            psB = tctx.enter_context(tc.psum_pool(name="psB", bufs=3))
-            psC = tctx.enter_context(tc.psum_pool(name="psC", bufs=2))
-            cxs = tailp.tile([P, NB, H], BF16, name="cxs")
-            nc.sync.dma_start(out=cxs[:], in_=cx.rearrange("(r p) h -> p r h", p=P))
-            cTall = tailp.tile([P, 8, B], F32, name="cTall")
-            soall = tailp.tile([P, 8, B], F32, name="soall")
-            wcb = tailp.tile([P, H], BF16, name="wcb")
-            bcb = tailp.tile([P, H], BF16, name="bcb")
-            SEQ = [(hb, q) for hb in range(8) for q in (2, 0, 1)]
-            NJ = len(SEQ)
-            aTs = {}
-            bTs = {}
-            Xs = {}
-            gs = {}
-            cxTs = {}
+            def normalise_hidden_half(hb):
+                for bt in range(NBT):
+                    cols = u_hid[:, bt * NCOL:(bt + 1) * NCOL].rearrange("p (q h) -> p q h", q=4)[:, :, hb * P:(hb + 1) * P]
+                    nc.vector.tensor_scalar(out=cols, in0=cols, scalar1=scal_hid[0][:, bt:bt + 1],
+                                            scalar2=scal_hid[1][:, bt:bt + 1], op0=ALU.subtract, op1=ALU.mult)
 
-            def flat(t):
-                return t[:].rearrange("p b c -> p (b c)")
-
-            def n_norm(hb):
-                for bt in range(NB):
-                    ap = Vt[:, bt * NCOL:(bt + 1) * NCOL].rearrange("p (q h) -> p q h", q=4)[:, :, hb * P:(hb + 1) * P]
-                    nc.vector.tensor_scalar(out=ap, in0=ap, scalar1=st["h"][0][:, bt:bt + 1],
-                                            scalar2=st["h"][1][:, bt:bt + 1], op0=ALU.subtract, op1=ALU.mult)
-
-            def t_to(key, src, pool, nm, store):
+            def columns_to_partitions(key, src, pool, store):
                 (hb, q) = key
-                store[key] = pool.tile([P, NB, P], F32, name=nm)
-                for bt in range(NB):
-                    col = bt * NCOL + q * H + hb * P
-                    nc.tensor.transpose(store[key][:, bt, :], src[:, col:col + P], ident_f[:])
+                store[key] = pool.tile([P, NBT, P], F32, name="turned")
+                for bt in range(NBT):
+                    first = bt * NCOL + q * H + hb * P
+                    nc.tensor.transpose(store[key][:, bt, :], src[:, first:first + P], ident_f[:])
 
-            def t_cx(hb):
-                cxTs[hb] = psC.tile([P, NB, P], BF16, name="cxT")
-                for bt in range(NB):
-                    nc.tensor.transpose(cxTs[hb][:, bt, :], cxs[:, bt, hb * P:(hb + 1) * P], ident_b[:])
+            def turn_cx(hb):
+                cxT[hb] = ps_c.tile([P, NBT, P], BF16, name="turned")
+                for bt in range(NBT):
+                    nc.tensor.transpose(cxT[hb][:, bt, :], cx_rows[:, bt, hb * P:(hb + 1) * P], ident_b[:])
 
-            def s_x(key):
+            def hidden_part(key):
                 (hb, q) = key
-                m = q * 8 + hb
-                if q == 3:
-                    Xs[key] = soall[:, hb, :]
+                m = q * NHB + hb
+                if q == GATE_O:
+                    hid_part[key] = outT[:, hb, :]
                 else:
-                    xt = xp.tile([P, B], F32, name="X")
-                    Xs[key] = xt[:]
-                if key in XV:
-                    nc.vector.tensor_scalar(out=Xs[key], in0=flat(bTs[key]), scalar1=cTf[:, 64 + m:65 + m],
-                                            scalar2=bsumT[:, m:m + 1], op0=ALU.mult, op1=ALU.add)
-                else:
-                    nc.scalar.activation(out=Xs[key], in_=flat(bTs[key]), func=ACT.Identity,
-                                         scale=cTf[:, 64 + m:65 + m], bias=bsumT[:, m:m + 1])
+                    t = part_pool.tile([P, B], F32, name="part")
+                    hid_part[key] = t[:]
+                nc.scalar.activation(out=hid_part[key], in_=flat(hid_T[key]), func=ACT.Identity,
+                                     scale=vecT_f[:, COL_LN_H_W + m:COL_LN_H_W + m + 1], bias=shiftT[:, m:m + 1])
 
-            def v_m(key):
+            def pre_activation(key):
                 (hb, q) = key
-                m = q * 8 + hb
-                if q == 3:
-                    gs[key] = soall[:, hb, :]
+                m = q * NHB + hb
+                if q == GATE_O:
+                    gate[key] = outT[:, hb, :]
                 else:
-                    gt = gp.tile([P, B], F32, name="g%d" % q)
-                    gs[key] = gt[:]
-                nc.vector.scalar_tensor_tensor(out=gs[key], in0=flat(aTs[key]), scalar=cTf[:, 32 + m:33 + m],
-                                               in1=Xs[key], op0=ALU.mult, op1=ALU.add)
+                    t = gate_pool.tile([P, B], F32, name="gate%d" % q)
+                    gate[key] = t[:]
+                nc.vector.scalar_tensor_tensor(out=gate[key], in0=flat(in_T[key]),
+                                               scalar=vecT_f[:, COL_LN_I_W + m:COL_LN_I_W + m + 1], in1=hid_part[key],
+                                               op0=ALU.mult, op1=ALU.add)
 
-            def s_act(key):
-                nc.scalar.activation(out=gs[key], in_=gs[key], func=(ACT.Tanh if key[1] == 1 else ACT.Sigmoid))
+            def activate(key):
+                nc.scalar.activation(out=gate[key], in_=gate[key], func=(ACT.Tanh if key[1] == GATE_J else ACT.Sigmoid))
 
-            def v_p(hb):
-                nc.vector.tensor_tensor(out=gs[(hb, 2)], in0=gs[(hb, 2)], in1=flat(cxTs[hb]), op=ALU.mult)
+            def forget_times_cx(hb):
+                nc.vector.tensor_tensor(out=gate[(hb, GATE_F)], in0=gate[(hb, GATE_F)], in1=flat(cxT[hb]), op=ALU.mult)
 
-            def g_qc(hb):
-                eng = nc.gpsimd if hb < GLAST else nc.vector
-                eng.tensor_tensor(out=gs[(hb, 0)], in0=gs[(hb, 0)], in1=gs[(hb, 1)], op=ALU.mult)
-                eng.tensor_tensor(out=cTall[:, hb, :], in0=gs[(hb, 2)], in1=gs[(hb, 0)], op=ALU.add)
+            def new_cell(hb):
+                engine = nc.gpsimd if hb < NHB - 1 else nc.vector
+                engine.tensor_tensor(out=gate[(hb, GATE_I)], in0=gate[(hb, GATE_I)], in1=gate[(hb, GATE_J)], op=ALU.mult)
+                engine.tensor_tensor(out=cellT[:, hb, :], in0=gate[(hb, GATE_F)], in1=gate[(hb, GATE_I)], op=ALU.add)
 
-            def bc_tail(col0, dst):
-                bank = psC.tile([P, 8, P], BF16, name="cxT")
-                for j in range(8):
-                    nc.tensor.transpose(bank[:, j, :], cT[:, col0 + j:col0 + j + 1].to_broadcast([P, P]), ident_b[:])
-                nc.scalar.copy(out=dst, in_=bank[:].rearrange("p j c -> p (j c)"))
+            def spread_row(col, dst):
+                bank = ps_c.tile([P, 8, P], BF16, name="turned")
+                for m in range(8):
+                    nc.tensor.transpose(bank[:, m, :], vecT[:, col + m:col + m + 1].to_broadcast([P, P]), ident_b[:])
+                nc.scalar.copy(out=dst, in_=bank[:].rearrange("p m c -> p (m c)"))
 
-            bc_tail(96, wcb[:])
-            bc_tail(104, bcb[:])
-            t_to(SEQ[0], Ut, psA, "aT", aTs)
-            t_to(SEQ[1], Ut, psA, "aT", aTs)
-            n_norm(0)
-            for j in range(-2, NJ + 3):
-                if 0 <= j + 2 < NJ:
-                    key = SEQ[j + 2]
-                    if j + 2 >= 2:
-                        t_to(key, Ut, psA, "aT", aTs)
-                    t_to(key, Vt, psB, "bT", bTs)
-                    if (j + 2) % 3 == 2:
-                        t_to((key[0], 3), Vt, psB, "bT", bTs)
-                        t_cx(key[0])
-                if 0 <= j + 1 < NJ:
-                    s_x(SEQ[j + 1])
-                if 0 <= j - 1 < NJ:
-                    s_act(SEQ[j - 1])
-                    if (j - 1) % 3 == 2:
-                        g_qc(SEQ[j - 1][0])
-                if 0 <= j < NJ:
-                    if j % 3 == 2:
-                        s_x((SEQ[j][0], 3))
-                    v_m(SEQ[j])
-                    if j % 3 == 0 and SEQ[j][0] + 1 < 8:
-                        n_norm(SEQ[j][0] + 1)
-                    if j % 3 == 2:
-                        v_p(SEQ[j][0])
+            items = [(hb, q) for hb in range(NHB) for q in (GATE_F, GATE_I, GATE_J)]
+            spread_row(COL_LN_C_W, ln_c_w_rows[:])
+            spread_row(COL_LN_C_B, ln_c_b_rows[:])
+            columns_to_partitions(items[0], u_in, ps_a, in_T)
+            columns_to_partitions(items[1], u_in, ps_a, in_T)
+            normalise_hidden_half(0)
+            for t in range(-2, len(items) + 1):
+                if t + 2 < len(items):
+                    key = items[t + 2]
+                    if t + 2 >= 2:
+                        columns_to_partitions(key, u_in, ps_a, in_T)
+                    columns_to_partitions(key, u_hid, ps_b, hid_T)
+                    if key[1] == GATE_J:
+                        columns_to_partitions((key[0], GATE_O), u_hid, ps_b, hid_T)
+                        turn_cx(key[0])
+                if 0 <= t + 1 < len(items):
+                    hidden_part(items[t + 1])
+                if t >= 1:
+                    activate(items[t - 1])
+                    if items[t - 1][1] == GATE_J:
+                        new_cell(items[t - 1][0])
+                if 0 <= t < len(items):
+                    (hb, q) = items[t]
+                    if q == GATE_J:
+                        hidden_part((hb, GATE_O))
+                    pre_activation(items[t])
+                    if q == GATE_F and hb + 1 < NHB:
+                        normalise_hidden_half(hb + 1)
+                    if q == GATE_J:
+                        forget_times_cx(hb)
 
-            mec = keep.tile([P, NB], F32, name="mec")
-            exc = keep.tile([P, NB], F32, name="exc")
-            nvc = keep.tile([P, NB], F32, name="nvc")
-            rsc = keep.tile([P, NB], F32, name="rsc")
-            cbs = {}
-            sbs = {}
+            cell_sum = keep.tile([P, NBT, 2], F32, name="cell_sum")
+            cell_sq = keep.tile([P, NBT, 2], F32, name="cell_sq")
+            cell_mean = keep.tile([P, NBT], F32, name="cell_mean")
+            cell_msq = keep.tile([P, NBT], F32, name="cell_msq")
+            cell_var = keep.tile([P, NBT], F32, name="cell_var")
+            cell_rstd = keep.tile([P, NBT], F32, name="cell_rstd")
+            cell_rows = {}
+            out_rows = {}
 
-            def cyr(bt):
-                return Ut[:, bt * NCOL:bt * NCOL + H]
+            def cy_of(bt):
+                return u_in[:, bt * NCOL:bt * NCOL + H]
 
-            def tcr(bt):
-                return Ut[:, bt * NCOL + H:bt * NCOL + 2 * H]
+            def hy_of(bt):
+                return u_in[:, bt * NCOL + H:bt * NCOL + 2 * H]
 
-            def e_back1(bt, hf, src, pool, nm, store):
-                t = pool.tile([P, NB, P], F32, name=nm)
-                store[(bt, hf)] = t
+            def rows_to_partitions(bt, hf, src, pool, store):
+                store[(bt, hf)] = pool.tile([P, 4, P], F32, name="turned")
                 for i in range(4):
-                    nc.tensor.transpose(t[:, i, :], src[:, 4 * hf + i, bt * P:(bt + 1) * P], ident_f[:])
+                    nc.tensor.transpose(store[(bt, hf)][:, i, :], src[:, 4 * hf + i, bt * P:(bt + 1) * P], ident_f[:])
 
-            def e_sums(bt, hf):
-                if True:
-                    nc.scalar.activation(out=junk[:, 0:CH], in_=flat(cbs[(bt, hf)]), func=ACT.Copy, scale=1.0 / H,
-                                         accum_out=sumC[:, bt, hf:hf + 1])
-                    nc.scalar.activation(out=junk[:, CH:2 * CH], in_=flat(cbs[(bt, hf)]), func=ACT.Square,
-                                         scale=1.0 / 32.0, accum_out=sqC[:, bt, hf:hf + 1])
+            def cell_sums(bt, hf):
+                nc.scalar.activation(out=unused[:, 0:CH], in_=flat(cell_rows[(bt, hf)]), func=ACT.Copy, scale=1.0 / H,
+                                     accum_out=cell_sum[:, bt, hf:hf + 1])
+                nc.scalar.activation(out=unused[:, CH:2 * CH], in_=flat(cell_rows[(bt, hf)]), func=ACT.Square,
+                                     scale=1.0 / 32.0, accum_out=cell_sq[:, bt, hf:hf + 1])
 
-            def e_st(bt, i):
-                c1 = slice(bt, bt + 1)
-                if i == 0:
-                    nc.vector.tensor_tensor(out=mec[:, c1], in0=sumC[:, bt, 0:1], in1=sumC[:, bt, 1:2], op=ALU.add)
-                    nc.vector.scalar_tensor_tensor(out=exc[:, c1], in0=sqC[:, bt, 0:1], scalar=EPS,
-                                                   in1=sqC[:, bt, 1:2], op0=ALU.add, op1=ALU.add)
-                if i == 1:
-                    nc.vector.scalar_tensor_tensor(out=nvc[:, c1], in0=mec[:, c1], scalar=mec[:, c1], in1=exc[:, c1],
-                                                   op0=ALU.mult, op1=ALU.subtract)
-                if i == 2:
-                    nc.vector.tensor_scalar(out=nvc[:, c1], in0=nvc[:, c1], scalar1=-1.0, scalar2=EPS,
+            def cell_scalars(bt, stage):
+                one = slice(bt, bt + 1)
+                if stage == 0:
+                    nc.vector.tensor_tensor(out=cell_mean[:, one], in0=cell_sum[:, bt, 0:1], in1=cell_sum[:, bt, 1:2],
+                                            op=ALU.add)
+                    nc.vector.scalar_tensor_tensor(out=cell_msq[:, one], in0=cell_sq[:, bt, 0:1], scalar=EPS,
+                                                   in1=cell_sq[:, bt, 1:2], op0=ALU.add, op1=ALU.add)
+                if stage == 1:
+                    nc.vector.scalar_tensor_tensor(out=cell_var[:, one], in0=cell_mean[:, one], scalar=cell_mean[:, one],
+                                                   in1=cell_msq[:, one], op0=ALU.mult, op1=ALU.subtract)
+                if stage == 2:
+                    nc.vector.tensor_scalar(out=cell_var[:, one], in0=cell_var[:, one], scalar1=-1.0, scalar2=EPS,
                                             op0=ALU.mult, op1=ALU.max)
-                    nc.gpsimd.tensor_tensor(out=rsc[:, c1], in0=nvc[:, c1], in1=neghalf[:, c1], op=ALU.pow)
+                    nc.gpsimd.tensor_tensor(out=cell_rstd[:, one], in0=cell_var[:, one], in1=neg_half[:, one], op=ALU.pow)
 
-            def e_a(bt, hf):
-                nc.vector.scalar_tensor_tensor(out=cyr(bt)[:, hf * CH:(hf + 1) * CH], in0=flat(cbs[(bt, hf)]),
-                                               scalar=mec[:, bt:bt + 1], in1=wcb[:, hf * CH:(hf + 1) * CH],
+            def centre_and_gain(bt, hf):
+                cols = slice(hf * CH, (hf + 1) * CH)
+                nc.vector.scalar_tensor_tensor(out=cy_of(bt)[:, cols], in0=flat(cell_rows[(bt, hf)]),
+                                               scalar=cell_mean[:, bt:bt + 1], in1=ln_c_w_rows[:, cols],
                                                op0=ALU.subtract, op1=ALU.mult)
 
-            def e_cy(bt):
-                nc.vector.scalar_tensor_tensor(out=cyr(bt), in0=cyr(bt), scalar=rsc[:, bt:bt + 1], in1=bcb[:],
-                                               op0=ALU.mult, op1=ALU.add)
-                nc.sync.dma_start(out=out_1[bt * P:(bt + 1) * P, :], in_=cyr(bt))
-                nc.scalar.activation(out=tcr(bt), in_=cyr(bt), func=ACT.Tanh)
+            def finish_cy(bt):
+                nc.vector.scalar_tensor_tensor(out=cy_of(bt), in0=cy_of(bt), scalar=cell_rstd[:, bt:bt + 1],
+                                               in1=ln_c_b_rows[:], op0=ALU.mult, op1=ALU.add)
+                nc.sync.dma_start(out=out_1[bt * P:(bt + 1) * P, :], in_=cy_of(bt))
+                nc.scalar.activation(out=hy_of(bt), in_=cy_of(bt), func=ACT.Tanh)
 
-            def e_hy(bt, hf):
-                nc.vector.tensor_tensor(out=tcr(bt)[:, hf * CH:(hf + 1) * CH], in0=tcr(bt)[:, hf * CH:(hf + 1) * CH],
-                                        in1=flat(sbs[(bt, hf)]), op=ALU.mult)
+            def finish_hy(bt, hf):
+                cols = slice(hf * CH, (hf + 1) * CH)
+                nc.vector.tensor_tensor(out=hy_of(bt)[:, cols], in0=hy_of(bt)[:, cols], in1=flat(out_rows[(bt, hf)]),
+                                        op=ALU.mult)
                 if hf == 1:
-                    nc.sync.dma_start(out=out_0[bt * P:(bt + 1) * P, :], in_=tcr(bt))
+                    nc.sync.dma_start(out=out_0[bt * P:(bt + 1) * P, :], in_=hy_of(bt))
 
-            def o_t(hb):
-                t_to((hb, 3), Ut, psC, "cxT", aTs)
+            def turn_out_gate(hb):
+                if hb < NHB:
+                    columns_to_partitions((hb, GATE_O), u_in, ps_c, in_T)
 
-            def o_m(hb):
-                v_m((hb, 3))
-
-            o_t(0)
-            o_t(1)
-            for t in range(NB + 1):
-                if t < NB:
-                    e_back1(t, 0, cTall, psA, "aT", cbs)
-                    e_sums(t, 0)
-                    o_m(2 * t)
-                if t > 0:
-                    e_st(t - 1, 0)
-                    e_a(t - 1, 0)
-                    e_st(t - 1, 1)
-                if t < NB:
-                    e_back1(t, 1, cTall, psA, "aT", cbs)
-                    e_sums(t, 1)
-                    if 2 * t + 2 < 8:
-                        o_t(2 * t + 2)
-                    o_m(2 * t + 1)
-                    if 2 * t + 3 < 8:
-                        o_t(2 * t + 3)
-                    s_act((2 * t, 3))
-                    s_act((2 * t + 1, 3))
-                if t > 0:
-                    e_a(t - 1, 1)
-                    e_st(t - 1, 2)
-                if t > 1:
-                    e_cy(t - 2)
-            e_back1(0, 0, soall, psB, "bT", sbs)
-            e_back1(0, 1, soall, psB, "bT", sbs)
-            e_hy(0, 0)
-            e_cy(NB - 1)
-            e_hy(0, 1)
-            for bt in range(1, NB):
-                e_back1(bt, 0, soall, psB, "bT", sbs)
-                e_back1(bt, 1, soall, psB, "bT", sbs)
-                e_hy(bt, 0)
-                e_hy(bt, 1)
+            turn_out_gate(0)
+            turn_out_gate(1)
+            for bt in range(NBT + 1):
+                if bt < NBT:
+                    rows_to_partitions(bt, 0, cellT, ps_a, cell_rows)
+                    cell_sums(bt, 0)
+                    pre_activation((2 * bt, GATE_O))
+                if bt > 0:
+                    cell_scalars(bt - 1, 0)
+                    centre_and_gain(bt - 1, 0)
+                    cell_scalars(bt - 1, 1)
+                if bt < NBT:
+                    rows_to_partitions(bt, 1, cellT, ps_a, cell_rows)
+                    cell_sums(bt, 1)
+                    turn_out_gate(2 * bt + 2)
+                    pre_activation((2 * bt + 1, GATE_O))
+                    turn_out_gate(2 * bt + 3)
+                    activate((2 * bt, GATE_O))
+                    activate((2 * bt + 1, GATE_O))
+                if bt > 0:
+                    centre_and_gain(bt - 1, 1)
+                    cell_scalars(bt - 1, 2)
+                if bt > 1:
+                    finish_cy(bt - 2)
+            for bt in range(NBT):
+                rows_to_partitions(bt, 0, outT, ps_b, out_rows)
+                rows_to_partitions(bt, 1, outT, ps_b, out_rows)
+                finish_hy(bt, 0)
+                if bt == 0:
+                    finish_cy(NBT - 1)
+                finish_hy(bt, 1)

@@ -304,7 +304,7 @@ def tile_adaptivelstmcell_pb_kernel(
                     load_z(0, 1)
                     load_z(1, 1)
                 elif r == 0 and c + 1 < 2 * NCH:
-                    transpose_words(c + 1, raw[c + 1][:], 3, second)
+                    transpose_words(c + 1, raw[c + 1][:], 3, "scalar")
                     load_weights(c + 4)
                 elif r > 0 and c + 2 < 2 * NCH:
                     transpose_words(c + 2, raw[c + 2][:], r - 1, ("scalar", second, "scalar")[r - 1])

@@ -84,17 +84,21 @@ def tile_adaptivelstmcell_pb_kernel(
             work = keep.tile([P, NBT], F32, name="work_" + name)
             var = keep.tile([P, NBT], F32, name="var_" + name)
             rstd = keep.tile([P, NBT], F32, name="rstd_" + name)
+            neg_mean = keep.tile([P, NBT], F32, name="neg_mean_" + name)
+            shift = keep.tile([P, NBT], F32, name="shift_" + name)
             if extra is None:
                 nc.vector.tensor_scalar(out=mean[:], in0=total, scalar1=1.0 / count, scalar2=None, op0=ALU.mult)
             else:
                 nc.vector.tensor_scalar(out=mean[:], in0=total, scalar1=extra, scalar2=1.0 / count,
                                         op0=ALU.add, op1=ALU.mult)
             nc.vector.tensor_tensor(out=work[:], in0=mean[:], in1=mean[:], op=ALU.mult)
+            nc.vector.tensor_scalar(out=neg_mean[:], in0=mean[:], scalar1=-1.0, scalar2=None, op0=ALU.mult)
             nc.vector.scalar_tensor_tensor(out=var[:], in0=total_sq, scalar=1.0 / count, in1=work[:],
                                            op0=ALU.mult, op1=ALU.subtract)
             nc.vector.tensor_scalar(out=var[:], in0=var[:], scalar1=0.0, scalar2=EPS, op0=ALU.max, op1=ALU.add)
             nc.gpsimd.tensor_tensor(out=rstd[:], in0=var[:], in1=neg_half[:], op=ALU.pow)
-            return (mean, rstd)
+            nc.gpsimd.tensor_tensor(out=shift[:], in0=neg_mean[:], in1=rstd[:], op=ALU.mult)
+            return (mean, rstd, shift)
 
         def half_scalars(half):
             total = keep.tile([P, NBT], F32, name="total%d" % half)
@@ -345,12 +349,12 @@ def tile_adaptivelstmcell_pb_kernel(
                 nc.scalar.activation(out=unused[:, 0:CH], in_=u, func=ACT.Square,
                                      accum_out=row_sq[:, half, bt, c % NCH:c % NCH + 1])
 
-            def normalise_input_half(i):
-                bt = i % NBT
-                first = bt * NCOL + (i // NBT) * H
-                nc.vector.tensor_scalar(out=u_in[:, first:first + H], in0=u_in[:, first:first + H],
-                                        scalar1=scal_in[0][:, bt:bt + 1], scalar2=scal_in[1][:, bt:bt + 1],
-                                        op0=ALU.subtract, op1=ALU.mult)
+            def normalise_input_half():
+                for i in range(NCH):
+                    for bt in range(NBT):
+                        cols = u_in[:, bt * NCOL + i * CH:bt * NCOL + (i + 1) * CH]
+                        nc.gpsimd.tensor_scalar(out=cols, in0=cols, scalar1=scal_in[1][:, bt:bt + 1],
+                                                scalar2=scal_in[2][:, bt:bt + 1], op0=ALU.mult, op1=ALU.add)
 
             FIRST_HID = NCH * NBT
             scal_in = None
@@ -383,12 +387,11 @@ def tile_adaptivelstmcell_pb_kernel(
                     sum_squares(n - 3)
                 quantise_in_step(n)
                 nc.vector.tensor_tensor(out=u, in0=xh[:], in1=alpha_sb[n][:], op=ALU.mult)
-                if FIRST_HID + 3 <= n < FIRST_HID + 3 + 4 * NBT:
-                    normalise_input_half(n - FIRST_HID - 3)
                 if n >= 1:
                     add_beta(n - 1)
                 if n == FIRST_HID + 2:
                     scal_in = half_scalars(0)
+                    normalise_input_half()
             add_beta(NUNIT - 1)
             for n in range(NUNIT - 3, NUNIT):
                 sum_squares(n)

from contextlib import ExitStack

import concourse.mybir as mybir
from concourse.masks import make_identity

F32 = mybir.dt.float32
BF16 = mybir.dt.bfloat16
U32 = mybir.dt.uint32
U8 = mybir.dt.uint8
FP8X4 = mybir.dt.float8_e4m3fn_x4
ALU = mybir.AluOpType
ACT = mybir.ActivationFunctionType
AX = mybir.AxisListType

P = 128
B = 512
K = 1024
H = 1024
NBT = B // P
NCOL = 4 * H
CH = 512
NCH = NCOL // CH
NUNIT = 2 * NCH * NBT
NHB = H // P
EPS = 1e-5
GATE_I = 0
GATE_J = 1
GATE_F = 2
GATE_O = 3

COL_B_IH = 0
COL_LN_I_W = 32
COL_LN_H_W = 64
COL_LN_C_W = 96
COL_LN_C_B = 104
COL_LN_I_B = 128
COL_LN_H_B = 160

FLOPS = 2 * 2 * B * NCOL * K + 16 * 2 * B * H * 128


def tile_adaptivelstmcell_pb_kernel(
    tc, x, hx, cx, zw, zb, w_ih, w_hh, b_ih, b_hh, norm_alpha_w, bias_beta_w,
    ln_i_w, ln_i_b, ln_h_w, ln_h_b, ln_c_w, ln_c_b, out_0, out_1,
):
    nc = tc.nc
    with ExitStack() as whole:
        whole.enter_context(tc.manual_schedule())
        keep = whole.enter_context(tc.tile_pool(name="keep", bufs=1))

        u_in = keep.tile([P, NBT * NCOL], F32, name="u_in")
        u_hid = keep.tile([P, NBT * NCOL], F32, name="u_hid")
        ident_f = keep.tile([P, P], F32, name="ident_f")
        ident_b = keep.tile([P, P], BF16, name="ident_b")
        act_words = [keep.tile([P, 2, B], U32, name="act_words%d" % h, align_bytes=64) for h in range(2)]
        act_scales = [keep.tile([P, 2, B], U8, name="act_scales%d" % h, align_bytes=64) for h in range(2)]
        zT = [keep.tile([P, 8, B], BF16, name="zT%d" % i) for i in range(2)]
        b_hh_rows = keep.tile([P, CH], BF16, name="b_hh_rows")
        vec_rows = keep.tile([P, 2, P], BF16, name="vec_rows")
        vecT = keep.tile([P, 2 * P], BF16, name="vecT")
        vecT_f = keep.tile([P, 2 * P], F32, name="vecT_f")
        shiftT = keep.tile([P, 32], F32, name="shiftT")
        neg_half = keep.tile([P, NBT], F32, name="neg_half")
        warm = keep.tile([P, 1], F32, name="warm")
        row_sum = keep.tile([P, 2, NBT, NCH], F32, name="row_sum")
        row_sq = keep.tile([P, 2, NBT, NCH], F32, name="row_sq")
        bias_sum = keep.tile([P, NCH], F32, name="bias_sum")
        unused = keep.tile([P, H], BF16, name="unused")

        def copy_on(engine, out, in_):
            if engine == "scalar":
                nc.scalar.copy(out=out, in_=in_)
            else:
                nc.vector.tensor_copy(out=out, in_=in_)

        def rows_on_partitions(ap2d):
            return ap2d.rearrange("(r p) k -> p r k", p=P)

        def flat(t):
            return t[:].rearrange("p b c -> p (b c)")

        def layer_norm_scalars(name, total, total_sq, count, extra):
            mean = keep.tile([P, NBT], F32, name="mean_" + name)
            work = keep.tile([P, NBT], F32, name="work_" + name)
            var = keep.tile([P, NBT], F32, name="var_" + name)
            rstd = keep.tile([P, NBT], F32, name="rstd_" + name)
            neg_mean = keep.tile([P, NBT], F32, name="neg_mean_" + name)
            shift = keep.tile([P, NBT], F32, name="shift_" + name)
            if extra is None:
                nc.vector.tensor_scalar(out=mean[:], in0=total, scalar1=1.0 / count, scalar2=None, op0=ALU.mult)
            else:
                nc.vector.tensor_scalar(out=mean[:], in0=total, scalar1=extra, scalar2=1.0 / count,
                                        op0=ALU.add, op1=ALU.mult)
            nc.vector.tensor_tensor(out=work[:], in0=mean[:], in1=mean[:], op=ALU.mult)
            nc.vector.tensor_scalar(out=neg_mean[:], in0=mean[:], scalar1=-1.0, scalar2=None, op0=ALU.mult)
            nc.vector.scalar_tensor_tensor(out=var[:], in0=total_sq, scalar=1.0 / count, in1=work[:],
                                           op0=ALU.mult, op1=ALU.subtract)
            nc.vector.tensor_scalar(out=var[:], in0=var[:], scalar1=0.0, scalar2=EPS, op0=ALU.max, op1=ALU.add)
            nc.gpsimd.tensor_tensor(out=rstd[:], in0=var[:], in1=neg_half[:], op=ALU.pow)
            nc.gpsimd.tensor_tensor(out=shift[:], in0=neg_mean[:], in1=rstd[:], op=ALU.mult)
            return (mean, rstd, shift)

        def half_scalars(half):
            total = keep.tile([P, NBT], F32, name="total%d" % half)
            total_sq = keep.tile([P, NBT], F32, name="total_sq%d" % half)
            nc.vector.tensor_reduce(out=total[:], in_=row_sum[:, half, :, :], axis=AX.X, op=ALU.add)
            nc.vector.tensor_reduce(out=total_sq[:], in_=row_sq[:, half, :, :], axis=AX.X, op=ALU.add)
            extra = None
            if half == 0:
                bias_total = keep.tile([P, 1], F32, name="bias_total")
                nc.vector.tensor_reduce(out=bias_total[:], in_=bias_sum[:], axis=AX.X, op=ALU.add)
                extra = bias_total[:]
            return layer_norm_scalars("half%d" % half, total[:], total_sq[:], NCOL, extra)

        nc.vector.memset(neg_half[:], -0.5)
        nc.scalar.activation(out=warm[:], in_=neg_half[:, 0:1], func=ACT.Sigmoid)
        nc.vector.memset(vec_rows[:], 0.0)
        nc.vector.memset(b_hh_rows[:], 0.0)
        make_identity(nc, ident_f[:])
        make_identity(nc, ident_b[:])

        with ExitStack() as stream:
            ps_t = stream.enter_context(tc.psum_pool(name="ps_t", bufs=2))
            ps_xh = stream.enter_context(tc.psum_pool(name="ps_xh", bufs=2))
            ps_alpha = stream.enter_context(tc.psum_pool(name="ps_alpha", bufs=2))
            ps_beta = stream.enter_context(tc.psum_pool(name="ps_beta", bufs=2))
            raw_pool = stream.enter_context(tc.tile_pool(name="raw_pool", bufs=3))
            hyper_raw_pool = stream.enter_context(tc.tile_pool(name="hyper_raw_pool", bufs=2))
            grouped_pool = stream.enter_context(tc.tile_pool(name="grouped_pool", bufs=3))
            mx_pool = stream.enter_context(tc.tile_pool(name="mx_pool", bufs=2))
            hyper_pool = stream.enter_context(tc.tile_pool(name="hyper_pool", bufs=2))
            alpha_pool = stream.enter_context(tc.tile_pool(name="alpha_pool", bufs=3))
            bias_pool = stream.enter_context(tc.tile_pool(name="bias_pool", bufs=2))

            def staged_words(i):
                return u_hid[:, i * 2048:(i + 1) * 2048]

            def staged_z(i, part):
                first = 4096 + (2 * i + part) * 1024
                return u_hid[:, first:first + 1024].bitcast(BF16).rearrange("p (r k) -> p r k", r=NBT)

            z_rows = [rows_on_partitions(z.rearrange("b s a -> b (s a)")) for z in (zw, zb)]

            def load_words(dst, src):
                nc.sync.dma_start(out=dst.bitcast(BF16).rearrange("p (r k) -> p r k", r=4), in_=rows_on_partitions(src))

            def load_z(i, part):
                nc.sync.dma_start(out=staged_z(i, part), in_=z_rows[i][:, :, 512 * part:512 * (part + 1)])

            raw = {}
            hyper_raw = {}

            def load_weights(c):
                if c < 2 * NCH:
                    w = w_ih if c < NCH else w_hh
                    raw[c] = raw_pool.tile([P, 2048], F32, name="raw")
                    load_words(raw[c][:], w[(c % NCH) * CH:(c % NCH + 1) * CH, :])

            def load_hyper(s):
                if s < 8:
                    ra = hyper_raw_pool.tile([P, 8, P], BF16, name="raw_alpha")
                    rb = hyper_raw_pool.tile([P, 8, P], BF16, name="raw_beta")
                    nc.sync.dma_start(out=ra[:], in_=norm_alpha_w[s, :, :].rearrange("(r p) a -> p r a", p=P))
                    nc.sync.dma_start(out=rb[:], in_=bias_beta_w[s, :, :].rearrange("(r p) a -> p r a", p=P))
                    hyper_raw[s] = (ra, rb)

            waiting = []
            grouped = {}
            w_words = {}
            w_scales = {}
            hyper = {}
            bias_rows = {}

            def copy_waiting():
                for (engine, out, in_, accum_out) in waiting:
                    if accum_out is None:
                        copy_on(engine, out, in_)
                    else:
                        nc.scalar.activation(out=out, in_=in_, func=ACT.Copy, accum_out=accum_out)
                waiting[:] = []

            def new_bank(shape, dtype):
                if len(waiting) == 2:
                    copy_waiting()
                return ps_t.tile(shape, dtype, name="bank")

            def transpose_words(operand, src, j, engine):
                g = j // 2
                h = j % 2
                if h == 0:
                    grouped[(operand, g)] = grouped_pool.tile([P, 4 * CH], BF16, name="grouped", align_bytes=64)
                bank = new_bank([P, 2, 2, P], F32)
                for u in range(2):
                    for r in range(2):
                        first = (2 * h + r) * 512 + 256 * g + 128 * u
                        nc.tensor.transpose(bank[:, u, r, :], src[:, first:first + P], ident_f[:])
                pairs = grouped[(operand, g)][:].bitcast(F32).rearrange("p (n u) -> p n u", u=2)
                waiting.append((engine, pairs[:, 256 * h:256 * (h + 1), :], bank[:].rearrange("p u r c -> p (r c) u"), None))

            def quantise(operand, g, words, scales):
                nc.vector.quantize_mx(out=words[:, g, :].bitcast(FP8X4), scales=scales[:, g, :],
                                      in_=grouped[(operand, g)][:])

            def transpose_z(i, part, pair, engine):
                src = staged_z(i, part)
                bank = new_bank([P, 4, 2, P], BF16)
                for s in range(4):
                    for t in range(2):
                        nc.tensor.transpose(bank[:, s, t, :], src[:, 2 * pair + t, s * P:(s + 1) * P], ident_b[:])
                waiting.append((engine, zT[i][:, 4 * part:4 * part + 4, 256 * pair:256 * (pair + 1)],
                                bank[:].rearrange("p s t b -> p s (t b)"), None))

            def transpose_hyper(c):
                bank = new_bank([P, 2, 4, P], BF16)
                for i in range(2):
                    for r in range(4):
                        nc.tensor.transpose(bank[:, i, r, :], hyper_raw[c // 2][i][:, (c % 2) * 4 + r, :], ident_b[:])
                hyper[c] = hyper_pool.tile([P, 2, CH], BF16, name="hyper")
                waiting.append(("scalar", hyper[c][:], bank[:].rearrange("p i r c -> p i (r c)"), None))

            def transpose_vectors():
                bank = new_bank([P, 2, P], BF16)
                for i in range(2):
                    nc.tensor.transpose(bank[:, i, :], vec_rows[:, i, :], ident_b[:])
                nc.vector.tensor_copy(out=vecT[:], in_=bank[:].rearrange("p i c -> p (i c)"))
                nc.vector.tensor_tensor(out=shiftT[:], in0=vecT[:, COL_LN_I_B:COL_LN_I_B + 32],
                                        in1=vecT[:, COL_LN_H_B:COL_LN_H_B + 32], op=ALU.add)
                nc.vector.tensor_copy(out=vecT_f[:], in_=vecT[:])

            def spread_bias(c):
                bank = new_bank([P, 4, P], BF16)
                for m in range(4):
                    col = COL_B_IH + 4 * c + m
                    nc.tensor.transpose(bank[:, m, :], vecT[:, col:col + 1].to_broadcast([P, P]), ident_b[:])
                bias_rows[c] = bias_pool.tile([P, CH], BF16, name="bias_rows")
                waiting.append(("scalar", bias_rows[c][:], bank[:].rearrange("p m c -> p (m c)"), bias_sum[:, c:c + 1]))

            load_words(staged_words(0), x)
            load_weights(0)
            load_z(0, 0)
            load_z(1, 0)
            load_hyper(0)
            load_weights(1)
            for (i, row, vec) in ((0, COL_B_IH, b_ih), (0, COL_LN_I_W, ln_i_w), (0, COL_LN_H_W, ln_h_w),
                                  (0, COL_LN_C_W, ln_c_w), (0, COL_LN_C_B, ln_c_b),
                                  (1, COL_LN_I_B - P, ln_i_b), (1, COL_LN_H_B - P, ln_h_b)):
                nc.sync.dma_start(out=vec_rows[row:row + vec.shape[0] // P, i, :], in_=vec.rearrange("(m p) -> m p", p=P))
            nc.sync.dma_start(out=b_hh_rows[0:NCH, :], in_=b_hh.rearrange("(c n) -> c n", c=NCH))
            load_hyper(1)
            load_weights(2)

            def new_mx_tiles(c):
                w_words[c] = mx_pool.tile([P, 2, CH], U32, name="w_words", align_bytes=64)
                w_scales[c] = mx_pool.tile([P, 2, CH], U8, name="w_scales", align_bytes=64)

            for j in range(4):
                transpose_words("x", staged_words(0), j, ("scalar", "vector")[j % 2])
            copy_waiting()
            quantise("x", 0, act_words[0], act_scales[0])
            new_mx_tiles(0)
            for j in range(4):
                transpose_words(0, raw[0][:], j, ("scalar", "vector")[j % 2])
                if j == 1:
                    copy_waiting()
                    quantise("x", 1, act_words[0], act_scales[0])
            copy_waiting()
            quantise(0, 0, w_words[0], w_scales[0])
            load_weights(3)
            for i in range(2):
                transpose_z(i, 0, 0, "scalar")
                transpose_z(i, 0, 1, "vector")
                copy_waiting()
                if i == 0:
                    quantise(0, 1, w_words[0], w_scales[0])
            transpose_hyper(0)
            copy_waiting()

            alpha_ps = {}
            alpha_sb = {}
            beta_ps = {}

            def where(n):
                c = n // NBT
                bt = n % NBT
                half = c // NCH
                first = bt * NCOL + (c % NCH) * CH
                return (c, bt, half, (u_in, u_hid)[half][:, first:first + CH])

            def alpha_of(n):
                (c, bt, half, u) = where(n)
                alpha_ps[n] = ps_alpha.tile([P, CH], F32, name="alpha_ps")
                nc.tensor.matmul(alpha_ps[n][:], lhsT=zT[0][:, c // 2, bt * P:(bt + 1) * P], rhs=hyper[c][:, 0, :],
                                 start=True, stop=True)
                alpha_sb[n] = alpha_pool.tile([P, CH], F32, name="alpha_sb")
                nc.scalar.copy(out=alpha_sb[n][:], in_=alpha_ps[n][:])

            def banks_of_step(n):
                c = n // NBT
                r = n % NBT
                second = "vector" if c < NCH - 1 else "scalar"
                if n == 0:
                    transpose_vectors()
                    spread_bias(0)
                    for j in range(4):
                        transpose_words(1, raw[1][:], j, ("scalar", "vector")[j % 2])
                    load_weights(4)
                    load_words(staged_words(1), hx)
                    load_z(0, 1)
                    load_z(1, 1)
                elif r == 0 and c + 1 < 2 * NCH:
                    transpose_words(c + 1, raw[c + 1][:], 3, "scalar")
                    load_weights(c + 4)
                elif r > 0 and c + 2 < 2 * NCH:
                    transpose_words(c + 2, raw[c + 2][:], r - 1, ("scalar", second, "scalar")[r - 1])
                if r == 1 and c + 1 < 2 * NCH:
                    transpose_hyper(c + 1)
                    if c % 2 == 0:
                        load_hyper(c // 2 + 2)
                if r == 2 and c + 1 < NCH:
                    spread_bias(c + 1)
                if 3 <= c <= 6 and r in (0, 3):
                    e = 2 * (c - 3) + r // 3
                    if e < 4:
                        transpose_words("hx", staged_words(1), e, ("scalar", "vector")[e % 2])
                    else:
                        transpose_z((e - 4) // 2, 1, e % 2, ("scalar", "vector")[e % 2])

            def quantise_in_step(n):
                c = n // NBT
                r = n % NBT
                if c + 1 < 2 * NCH and n > 0:
                    if r == (1 if c == 0 else 0):
                        new_mx_tiles(c + 1)
                        quantise(c + 1, 0, w_words[c + 1], w_scales[c + 1])
                    if r == 2:
                        quantise(c + 1, 1, w_words[c + 1], w_scales[c + 1])
                if r == 1 and c in (4, 5):
                    quantise("hx", c - 4, act_words[1], act_scales[1])

            def add_beta(n):
                (c, bt, half, u) = where(n)
                nc.vector.scalar_tensor_tensor(out=u, in0=u, scalar=1.0, in1=beta_ps[n][:], op0=ALU.mult, op1=ALU.add,
                                               accum_out=row_sum[:, half, bt, c % NCH:c % NCH + 1])
                if half == 0:
                    nc.gpsimd.tensor_tensor(out=u, in0=u, in1=bias_rows[c][:], op=ALU.add)

            def sum_squares(n):
                (c, bt, half, u) = where(n)
                nc.scalar.activation(out=unused[:, 0:CH], in_=u, func=ACT.Square,
                                     accum_out=row_sq[:, half, bt, c % NCH:c % NCH + 1])

            def normalise_input_half():
                for i in range(NCH):
                    for bt in range(NBT):
                        cols = u_in[:, bt * NCOL + i * CH:bt * NCOL + (i + 1) * CH]
                        nc.gpsimd.tensor_scalar(out=cols, in0=cols, scalar1=scal_in[1][:, bt:bt + 1],
                                                scalar2=scal_in[2][:, bt:bt + 1], op0=ALU.mult, op1=ALU.add)

            FIRST_HID = NCH * NBT
            scal_in = None
            alpha_of(0)
            for n in range(NUNIT):
                (c, bt, half, u) = where(n)
                rows = slice(bt * P, (bt + 1) * P)
                xh = ps_xh.tile([P, CH], F32, name="xh")
                for g in range(2):
                    nc.tensor.matmul_mx(
                        out=xh[:],
                        lhsT=act_words[half][:, g, rows].bitcast(FP8X4),
                        lhsT_scale=act_scales[half][:, g, rows],
                        rhs=w_words[c][:, g, :].bitcast(FP8X4),
                        rhs_scale=w_scales[c][:, g, :],
                        start=(g == 0),
                        stop=(g == 1),
                    )
                copy_waiting()
                if n + 1 < NUNIT:
                    alpha_of(n + 1)
                banks_of_step(n)
                beta_ps[n] = ps_beta.tile([P, CH], F32, name="beta_ps")
                nc.tensor.matmul(beta_ps[n][:], lhsT=zT[1][:, c // 2, rows], rhs=hyper[c][:, 1, :], start=True,
                                 stop=(half == 0))
                if half == 1:
                    nc.tensor.matmul(beta_ps[n][:], lhsT=ident_b[:, c % NCH:c % NCH + 1].to_broadcast([P, P]),
                                     rhs=b_hh_rows[:], start=False, stop=True)
                if n >= 3:
                    sum_squares(n - 3)
                quantise_in_step(n)
                nc.vector.tensor_tensor(out=u, in0=xh[:], in1=alpha_sb[n][:], op=ALU.mult)
                if n >= 1:
                    add_beta(n - 1)
                if n == FIRST_HID + 2:
                    scal_in = half_scalars(0)
                    normalise_input_half()
            add_beta(NUNIT - 1)
            for n in range(NUNIT - 3, NUNIT):
                sum_squares(n)
            scal_hid = half_scalars(1)

        with ExitStack() as tail:
            tail_keep = tail.enter_context(tc.tile_pool(name="tail_keep", bufs=1))
            part_pool = tail.enter_context(tc.tile_pool(name="part_pool", bufs=3))
            gate_pool = tail.enter_context(tc.tile_pool(name="gate_pool", bufs=2))
            ps_a = tail.enter_context(tc.psum_pool(name="ps_a", bufs=3))
            ps_b = tail.enter_context(tc.psum_pool(name="ps_b", bufs=3))
            ps_c = tail.enter_context(tc.psum_pool(name="ps_c", bufs=2))
            cx_rows = tail_keep.tile([P, NBT, H], BF16, name="cx_rows")
            nc.sync.dma_start(out=cx_rows[:], in_=rows_on_partitions(cx))
            cellT = tail_keep.tile([P, NHB, B], F32, name="cellT")
            outT = tail_keep.tile([P, NHB, B], F32, name="outT")
            ln_c_w_rows = tail_keep.tile([P, H], BF16, name="ln_c_w_rows")
            ln_c_b_rows = tail_keep.tile([P, H], BF16, name="ln_c_b_rows")

            in_T = {}
            hid_T = {}
            hid_part = {}
            gate = {}
            cxT = {}

            def normalise_hidden_half(hb):
                for bt in range(NBT):
                    cols = u_hid[:, bt * NCOL:(bt + 1) * NCOL].rearrange("p (q h) -> p q h", q=4)[:, :, hb * P:(hb + 1) * P]
                    nc.vector.tensor_scalar(out=cols, in0=cols, scalar1=scal_hid[0][:, bt:bt + 1],
                                            scalar2=scal_hid[1][:, bt:bt + 1], op0=ALU.subtract, op1=ALU.mult)

            def columns_to_partitions(key, src, pool, store):
                (hb, q) = key
                store[key] = pool.tile([P, NBT, P], F32, name="turned")
                for bt in range(NBT):
                    first = bt * NCOL + q * H + hb * P
                    nc.tensor.transpose(store[key][:, bt, :], src[:, first:first + P], ident_f[:])

            def turn_cx(hb):
                cxT[hb] = ps_c.tile([P, NBT, P], BF16, name="turned")
                for bt in range(NBT):
                    nc.tensor.transpose(cxT[hb][:, bt, :], cx_rows[:, bt, hb * P:(hb + 1) * P], ident_b[:])

            def hidden_part(key):
                (hb, q) = key
                m = q * NHB + hb
                if q == GATE_O:
                    hid_part[key] = outT[:, hb, :]
                else:
                    t = part_pool.tile([P, B], F32, name="part")
                    hid_part[key] = t[:]
                nc.scalar.activation(out=hid_part[key], in_=flat(hid_T[key]), func=ACT.Identity,
                                     scale=vecT_f[:, COL_LN_H_W + m:COL_LN_H_W + m + 1], bias=shiftT[:, m:m + 1])

            def pre_activation(key):
                (hb, q) = key
                m = q * NHB + hb
                if q == GATE_O:
                    gate[key] = outT[:, hb, :]
                else:
                    t = gate_pool.tile([P, B], F32, name="gate%d" % q)
                    gate[key] = t[:]
                nc.vector.scalar_tensor_tensor(out=gate[key], in0=flat(in_T[key]),
                                               scalar=vecT_f[:, COL_LN_I_W + m:COL_LN_I_W + m + 1], in1=hid_part[key],
                                               op0=ALU.mult, op1=ALU.add)

            def activate(key):
                nc.scalar.activation(out=gate[key], in_=gate[key], func=(ACT.Tanh if key[1] == GATE_J else ACT.Sigmoid))

            def forget_times_cx(hb):
                nc.vector.tensor_tensor(out=gate[(hb, GATE_F)], in0=gate[(hb, GATE_F)], in1=flat(cxT[hb]), op=ALU.mult)

            def new_cell(hb):
                engine = nc.gpsimd if hb < NHB - 1 else nc.vector
                engine.tensor_tensor(out=gate[(hb, GATE_I)], in0=gate[(hb, GATE_I)], in1=gate[(hb, GATE_J)], op=ALU.mult)
                engine.tensor_tensor(out=cellT[:, hb, :], in0=gate[(hb, GATE_F)], in1=gate[(hb, GATE_I)], op=ALU.add)

            def spread_row(col, dst):
                bank = ps_c.tile([P, 8, P], BF16, name="turned")
                for m in range(8):
                    nc.tensor.transpose(bank[:, m, :], vecT[:, col + m:col + m + 1].to_broadcast([P, P]), ident_b[:])
                nc.scalar.copy(out=dst, in_=bank[:].rearrange("p m c -> p (m c)"))

            items = [(hb, q) for hb in range(NHB) for q in (GATE_F, GATE_I, GATE_J)]
            spread_row(COL_LN_C_W, ln_c_w_rows[:])
            spread_row(COL_LN_C_B, ln_c_b_rows[:])
            columns_to_partitions(items[0], u_in, ps_a, in_T)
            columns_to_partitions(items[1], u_in, ps_a, in_T)
            normalise_hidden_half(0)
            for t in range(-2, len(items) + 1):
                if t + 2 < len(items):
                    key = items[t + 2]
                    if t + 2 >= 2:
                        columns_to_partitions(key, u_in, ps_a, in_T)
                    columns_to_partitions(key, u_hid, ps_b, hid_T)
                    if key[1] == GATE_J:
                        columns_to_partitions((key[0], GATE_O), u_hid, ps_b, hid_T)
                        turn_cx(key[0])
                if 0 <= t + 1 < len(items):
                    hidden_part(items[t + 1])
                if t >= 1:
                    activate(items[t - 1])
                    if items[t - 1][1] == GATE_J:
                        new_cell(items[t - 1][0])
                if 0 <= t < len(items):
                    (hb, q) = items[t]
                    if q == GATE_J:
                        hidden_part((hb, GATE_O))
                    pre_activation(items[t])
                    if q == GATE_F and hb + 1 < NHB:
                        normalise_hidden_half(hb + 1)
                    if q == GATE_J:
                        forget_times_cx(hb)

            cell_sum = keep.tile([P, NBT, 2], F32, name="cell_sum")
            cell_sq = keep.tile([P, NBT, 2], F32, name="cell_sq")
            cell_mean = keep.tile([P, NBT], F32, name="cell_mean")
            cell_msq = keep.tile([P, NBT], F32, name="cell_msq")
            cell_var = keep.tile([P, NBT], F32, name="cell_var")
            cell_rstd = keep.tile([P, NBT], F32, name="cell_rstd")
            cell_rows = {}
            out_rows = {}

            def cy_of(bt):
                return u_in[:, bt * NCOL:bt * NCOL + H]

            def hy_of(bt):
                return u_in[:, bt * NCOL + H:bt * NCOL + 2 * H]

            def rows_to_partitions(bt, hf, src, pool, store):
                store[(bt, hf)] = pool.tile([P, 4, P], F32, name="turned")
                for i in range(4):
                    nc.tensor.transpose(store[(bt, hf)][:, i, :], src[:, 4 * hf + i, bt * P:(bt + 1) * P], ident_f[:])

            def cell_sums(bt, hf):
                nc.scalar.activation(out=unused[:, 0:CH], in_=flat(cell_rows[(bt, hf)]), func=ACT.Copy, scale=1.0 / H,
                                     accum_out=cell_sum[:, bt, hf:hf + 1])
                nc.scalar.activation(out=unused[:, CH:2 * CH], in_=flat(cell_rows[(bt, hf)]), func=ACT.Square,
                                     scale=1.0 / 32.0, accum_out=cell_sq[:, bt, hf:hf + 1])

            def cell_scalars(bt, stage):
                one = slice(bt, bt + 1)
                if stage == 0:
                    nc.vector.tensor_tensor(out=cell_mean[:, one], in0=cell_sum[:, bt, 0:1], in1=cell_sum[:, bt, 1:2],
                                            op=ALU.add)
                    nc.vector.scalar_tensor_tensor(out=cell_msq[:, one], in0=cell_sq[:, bt, 0:1], scalar=EPS,
                                                   in1=cell_sq[:, bt, 1:2], op0=ALU.add, op1=ALU.add)
                if stage == 1:
                    nc.vector.scalar_tensor_tensor(out=cell_var[:, one], in0=cell_mean[:, one], scalar=cell_mean[:, one],
                                                   in1=cell_msq[:, one], op0=ALU.mult, op1=ALU.subtract)
                if stage == 2:
                    nc.vector.tensor_scalar(out=cell_var[:, one], in0=cell_var[:, one], scalar1=-1.0, scalar2=EPS,
                                            op0=ALU.mult, op1=ALU.max)
                    nc.gpsimd.tensor_tensor(out=cell_rstd[:, one], in0=cell_var[:, one], in1=neg_half[:, one], op=ALU.pow)

            def centre_and_gain(bt, hf):
                cols = slice(hf * CH, (hf + 1) * CH)
                nc.vector.scalar_tensor_tensor(out=cy_of(bt)[:, cols], in0=flat(cell_rows[(bt, hf)]),
                                               scalar=cell_mean[:, bt:bt + 1], in1=ln_c_w_rows[:, cols],
                                               op0=ALU.subtract, op1=ALU.mult)

            def finish_cy(bt):
                nc.vector.scalar_tensor_tensor(out=cy_of(bt), in0=cy_of(bt), scalar=cell_rstd[:, bt:bt + 1],
                                               in1=ln_c_b_rows[:], op0=ALU.mult, op1=ALU.add)
                nc.sync.dma_start(out=out_1[bt * P:(bt + 1) * P, :], in_=cy_of(bt))
                nc.scalar.activation(out=hy_of(bt), in_=cy_of(bt), func=ACT.Tanh)

            def finish_hy(bt, hf):
                cols = slice(hf * CH, (hf + 1) * CH)
                nc.vector.tensor_tensor(out=hy_of(bt)[:, cols], in0=hy_of(bt)[:, cols], in1=flat(out_rows[(bt, hf)]),
                                        op=ALU.mult)
                if hf == 1:
                    nc.sync.dma_start(out=out_0[bt * P:(bt + 1) * P, :], in_=hy_of(bt))

            def turn_out_gate(hb):
                if hb < NHB:
                    columns_to_partitions((hb, GATE_O), u_in, ps_c, in_T)

            turn_out_gate(0)
            turn_out_gate(1)
            for bt in range(NBT + 1):
                if bt < NBT:
                    rows_to_partitions(bt, 0, cellT, ps_a, cell_rows)
                    cell_sums(bt, 0)
                    pre_activation((2 * bt, GATE_O))
                if bt > 0:
                    cell_scalars(bt - 1, 0)
                    centre_and_gain(bt - 1, 0)
                    cell_scalars(bt - 1, 1)
                if bt < NBT:
                    rows_to_partitions(bt, 1, cellT, ps_a, cell_rows)
                    cell_sums(bt, 1)
                    turn_out_gate(2 * bt + 2)
                    pre_activation((2 * bt + 1, GATE_O))
                    turn_out_gate(2 * bt + 3)
                    activate((2 * bt, GATE_O))
                    activate((2 * bt + 1, GATE_O))
                if bt > 0:
                    centre_and_gain(bt - 1, 1)
                    cell_scalars(bt - 1, 2)
                if bt > 1:
                    finish_cy(bt - 2)
            for bt in range(NBT):
                rows_to_partitions(bt, 0, outT, ps_b, out_rows)
                rows_to_partitions(bt, 1, outT, ps_b, out_rows)
                finish_hy(bt, 0)
                if bt == 0:
                    finish_cy(NBT - 1)
                finish_hy(bt, 1)
